import numpy as np
import ml_dtypes


def mxq(x, axis, fmt="e4m3"):
    dtype, down = {"e4m3": (ml_dtypes.float8_e4m3fn, 7), "e5m2": (ml_dtypes.float8_e5m2, 14)}[fmt]
    v = np.moveaxis(np.asarray(x, np.float32).astype(ml_dtypes.bfloat16).astype(np.float64), axis, -1)
    blocks = v.reshape(v.shape[:-1] + (-1, 32))
    amax = np.abs(blocks).max(-1, keepdims=True)
    byte = np.maximum(np.where(amax > 0, np.frexp(amax)[1] - 1 + 127, 0) - down, 1)
    scale = np.exp2(byte - 127.0)
    codes = (blocks / scale).astype(np.float32).astype(dtype).astype(np.float64)
    return np.moveaxis((codes * scale).reshape(v.shape), -1, axis)


BF16 = ml_dtypes.bfloat16


def bf(x):
    return np.asarray(x, np.float32).astype(BF16)


def f64(x):
    return np.asarray(x).astype(np.float64)


B, C, H, W, G = 8, 128, 32, 32, 8
N = H * W
THRESHOLD = 16.0


def draw_x():
    q = np.linalg.qr(np.random.standard_normal((C, C)))[0]
    ia = np.random.randint(0, G, (B, N))
    ib = np.random.randint(0, G, (B, N)) + G
    codes = 0.55 * THRESHOLD * (q[:, ia] + q[:, ib]).transpose(1, 0, 2)
    noise = 0.212 * THRESHOLD / np.sqrt(C) * np.random.standard_normal((B, C, N))
    return (codes + noise).reshape(B, C, H, W)


def setup_inputs():
    return {"x": bf(draw_x()),
            "W_fc": bf(np.random.standard_normal((C, C)) * 2.0 / np.sqrt(C)),
            "b_fc": bf(np.random.standard_normal(C) * 0.2)}


def reference(x, W_fc, b_fc):
    xf = f64(x).reshape(B, C, N).transpose(0, 2, 1)
    sq = (xf * xf).sum(-1)
    d2 = sq[:, :, None] + sq[:, None, :] - 2.0 * (xf @ xf.transpose(0, 2, 1))
    dist = np.sqrt(np.maximum(d2, 0.0))
    inc = np.where(dist < THRESHOLD, 1.0, 0.0)
    incq = mxq(inc, 2, "e4m3")
    xe = xf @ f64(W_fc).T + f64(b_fc)
    deg_e = inc.sum(1)
    edge = incq @ mxq(xe, 1, "e4m3")
    edge = np.where(deg_e > 0, 1.0 / deg_e, 0.0)[:, :, None] * edge
    deg_v = inc.sum(2)
    vert = incq @ mxq(edge, 1, "e4m3")
    vert = np.where(deg_v > 0, 1.0 / deg_v, 0.0)[:, :, None] * vert
    out = vert + xf
    return out.transpose(0, 2, 1).reshape(B, C, H, W)

@@ -1,0 +1,330 @@
+from contextlib import ExitStack
+
+import concourse.mybir as mybir
+from concourse.masks import make_identity
+
+F32 = mybir.dt.float32
+BF16 = mybir.dt.bfloat16
+U32 = mybir.dt.uint32
+U8 = mybir.dt.uint8
+FP8X4 = mybir.dt.float8_e4m3fn_x4
+ALU = mybir.AluOpType
+ACT = mybir.ActivationFunctionType
+
+P = 128
+BATCH = 8
+PIXELS = 1024
+TILES = PIXELS // P
+PACK = 4
+PASSES = TILES // PACK
+BANK = 512
+THRESHOLD = 16.0
+STEPS = PASSES * TILES
+GRAM_RING = 3
+AHEAD = GRAM_RING - 1
+
+FLOPS = BATCH * (3 * 2 * PIXELS * PIXELS * P + 2 * PIXELS * P * P)
+
+
+def tile_hypercomputemodule_pa_t_kernel(tc, x, W_fc, b_fc, out):
+    nc = tc.nc
+    with ExitStack() as ctx:
+        consts = ctx.enter_context(tc.tile_pool(name="consts", bufs=1))
+        small = ctx.enter_context(tc.tile_pool(name="small", bufs=2))
+        work = ctx.enter_context(tc.tile_pool(name="work", bufs=2))
+        tables = ctx.enter_context(tc.tile_pool(name="tables", bufs=1))
+        incidence = ctx.enter_context(tc.tile_pool(name="incidence", bufs=2))
+        gram_banks = ctx.enter_context(tc.psum_pool(name="gram_banks", bufs=GRAM_RING))
+        prep_banks = ctx.enter_context(tc.psum_pool(name="prep_banks", bufs=2))
+        post_banks = ctx.enter_context(tc.psum_pool(name="post_banks", bufs=3))
+        ctx.enter_context(tc.manual_schedule())
+
+        x_sb = consts.tile([P, BATCH, PIXELS], BF16)
+        for b in range(BATCH):
+            nc.sync.dma_start(out=x_sb[:, b, :], in_=x[b].rearrange("c h w -> c (h w)"))
+        w_sb = consts.tile([P, P], BF16)
+        nc.scalar.dma_start(out=w_sb[:], in_=W_fc)
+        bias_rows = consts.tile([P, P], BF16)
+        nc.vector.memset(bias_rows[:], 0.0)
+        nc.scalar.dma_start(out=bias_rows[0:1, :], in_=b_fc.rearrange("(o c) -> o c", o=1))
+        ones_bf = consts.tile([P, P], BF16)
+        nc.vector.memset(ones_bf[:], 1.0)
+        ident_bf = consts.tile([P, P], BF16)
+        make_identity(nc, ident_bf[:])
+        ident_f32 = consts.tile([P, P], F32)
+        make_identity(nc, ident_f32[:])
+
+        w_ps = prep_banks.tile([P, P], BF16, tag="prep")
+        nc.tensor.transpose(w_ps[:], w_sb[:], ident_bf[:])
+        w_t = consts.tile([P, P], BF16)
+        nc.vector.tensor_copy(out=w_t[:], in_=w_ps[:])
+
+        ones_in = consts.tile([P, PACK * P], BF16, align_bytes=64)
+        nc.vector.memset(ones_in[:], 1.0)
+        xe_words = [consts.tile([P, PASSES, 2 * P], U32, align_bytes=64, name="xe_words%d" % s) for s in range(2)]
+        xe_scales = [consts.tile([P, PASSES, 2 * P], U8, align_bytes=64, name="xe_scales%d" % s) for s in range(2)]
+        for s in range(2):
+            for g in range(PASSES):
+                nc.vector.quantize_mx(
+                    out=xe_words[s][:, g, P : 2 * P].bitcast(FP8X4),
+                    scales=xe_scales[s][:, g, P : 2 * P],
+                    in_=ones_in[:],
+                )
+
+        live = {}
+
+        def pixel_tile(b, t):
+            return x_sb[:, b, t * P : (t + 1) * P]
+
+        def transpose_x(b, part):
+            xf_ps = prep_banks.tile([P, TILES, P], BF16, tag="prep")
+            for t in range(TILES):
+                nc.tensor.transpose(xf_ps[:, t, :], pixel_tile(b, t), ident_bf[:])
+            live["xf_ps", b] = xf_ps
+            live["squares", b] = work.tile([P, TILES, P], BF16, name="squares")
+            live["sq", b] = small.tile([P, TILES], F32, name="sq")
+
+        def square_sums(b, g):
+            for t in range(PACK * g, PACK * (g + 1)):
+                nc.scalar.activation(
+                    out=live["squares", b][:, t, :],
+                    in_=live["xf_ps", b][:, t, :],
+                    func=ACT.Square,
+                    accum_out=live["sq", b][:, t : t + 1],
+                )
+
+        def half_thresholds(b, part):
+            h_col = small.tile([P, TILES], F32)
+            nc.vector.tensor_scalar(
+                out=h_col[:],
+                in0=live["sq", b][:],
+                scalar1=0.5,
+                scalar2=-THRESHOLD * THRESHOLD / 4.0,
+                op0=ALU.mult,
+                op1=ALU.add,
+            )
+            live["h_col", b] = h_col
+            live["h_rep", b] = work.tile([P, TILES, P], F32, name="h_rep")
+            live["h_row", b] = work.tile([P, PIXELS], F32, name="h_row")
+
+        def repeat_h(b, g):
+            tiles_of_pass = slice(PACK * g, PACK * (g + 1))
+            nc.gpsimd.tensor_scalar(
+                out=live["h_rep", b][:, tiles_of_pass, :],
+                in0=live["h_col", b][:, tiles_of_pass].unsqueeze(2).to_broadcast([P, PACK, P]),
+                scalar1=1.0,
+                scalar2=0.0,
+                op0=ALU.mult,
+                op1=ALU.add,
+            )
+
+        def transpose_h(b, g):
+            h_ps = prep_banks.tile([P, PACK, P], F32, tag="prep")
+            for e in range(PACK):
+                nc.tensor.transpose(h_ps[:, e, :], live["h_rep", b][:, PACK * g + e, :], ident_f32[:])
+            live["h_ps", b, g] = h_ps
+
+        def copy_h(b, g):
+            nc.scalar.copy(
+                out=live["h_row", b][:, g * BANK : (g + 1) * BANK], in_=live["h_ps", b, g][:].rearrange("p e w -> p (e w)")
+            )
+
+        def table_rows(b, g, pair):
+            if pair == 0:
+                live["thresh", b, g] = tables.tile([P, PACK, PIXELS], F32, tag="thresh%d" % g, name="thresh")
+            thresh = live["thresh", b, g]
+            e = 2 * pair
+            t = PACK * g + e
+            nc.scalar.activation(
+                out=thresh[:, e, :], in_=live["h_row", b][:], func=ACT.Identity, bias=live["h_col", b][:, t : t + 1]
+            )
+            nc.gpsimd.tensor_scalar(
+                out=thresh[:, e + 1, :],
+                in0=live["h_row", b][:],
+                scalar1=1.0,
+                scalar2=live["h_col", b][:, t + 1 : t + 2],
+                op0=ALU.mult,
+                op1=ALU.add,
+            )
+
+        def table_first_pass(b, pair):
+            table_rows(b, 0, pair)
+
+        def table_second_pass(b, pair):
+            table_rows(b, 1, pair)
+
+        def project(b, g):
+            xe_ps = prep_banks.tile([P, PACK, P], F32, tag="prep")
+            for e in range(PACK):
+                nc.tensor.matmul(xe_ps[:, e, :], lhsT=ones_bf[:], rhs=bias_rows[:], start=True, stop=False)
+                nc.tensor.matmul(xe_ps[:, e, :], lhsT=pixel_tile(b, PACK * g + e), rhs=w_t[:], start=False, stop=True)
+            live["xe_ps", b, g] = xe_ps
+
+        def round_xe(b, g):
+            xe_in = work.tile([P, P, PACK], BF16, align_bytes=64)
+            nc.scalar.copy(out=xe_in[:], in_=live["xe_ps", b, g][:].rearrange("p e c -> p c e"))
+            live["xe_in", b, g] = xe_in
+
+        def quantise_xe(b, g):
+            nc.vector.quantize_mx(
+                out=xe_words[b % 2][:, g, 0:P].bitcast(FP8X4),
+                scales=xe_scales[b % 2][:, g, 0:P],
+                in_=live["xe_in", b, g][:].rearrange("p c e -> p (c e)"),
+            )
+
+        def gram_bank(b, i):
+            g, nb = divmod(i, TILES)
+            gram = gram_banks.tile([P, PACK, P], F32)
+            for e in range(PACK):
+                nc.tensor.matmul(
+                    gram[:, e, :], lhsT=pixel_tile(b, PACK * g + e), rhs=pixel_tile(b, nb), start=True, stop=True
+                )
+            live["gram", b, i] = gram
+
+        def compare(b, i):
+            g, nb = divmod(i, TILES)
+            cols = slice(nb * P, (nb + 1) * P)
+            if i == 0:
+                live["inc_words", b] = incidence.tile([P, PASSES, PIXELS], U32, align_bytes=64, name="inc_words")
+                live["inc_scales", b] = incidence.tile([P, PASSES, PIXELS], U8, align_bytes=64, name="inc_scales")
+            if nb == 0:
+                live["inc_in", b] = incidence.tile([P, PIXELS, PACK], BF16, align_bytes=64, name="inc_in")
+            inc_in = live["inc_in", b]
+            nc.vector.tensor_tensor(
+                out=inc_in[:, cols, :],
+                in0=live["gram", b, i][:].rearrange("p e w -> p w e"),
+                in1=live["thresh", b, g][:, :, cols].rearrange("p e w -> p w e"),
+                op=ALU.is_gt,
+            )
+            if nb == TILES - 1:
+                nc.vector.quantize_mx(
+                    out=live["inc_words", b][:, g, :].bitcast(FP8X4),
+                    scales=live["inc_scales", b][:, g, :],
+                    in_=inc_in[:].rearrange("p w e -> p (w e)"),
+                )
+
+        def inc_times(acc, b, t, rhs_words, rhs_scales):
+            cols = slice(t * P, (t + 1) * P)
+            for g in range(PASSES):
+                nc.tensor.matmul_mx(
+                    out=acc,
+                    lhsT=live["inc_words", b][:, g, cols].bitcast(FP8X4),
+                    lhsT_scale=live["inc_scales", b][:, g, cols],
+                    rhs=rhs_words[:, g, :].bitcast(FP8X4),
+                    rhs_scale=rhs_scales[:, g, :],
+                    start=(g == 0),
+                    stop=(g == PASSES - 1),
+                )
+
+        def edge_sums(b, pair):
+            edge_ps = post_banks.tile([P, 2, 2 * P], F32, tag="post")
+            for i in range(2):
+                inc_times(edge_ps[:, i, :], b, 2 * pair + i, xe_words[b % 2], xe_scales[b % 2])
+            live["edge_ps", b, pair] = edge_ps
+
+        def reciprocals(b, pair):
+            if pair == 0:
+                live["deg", b] = small.tile([P, TILES], F32, name="deg")
+                live["recip", b] = small.tile([P, TILES], F32, name="recip")
+                live["edge_f32", b] = work.tile([P, TILES, P], F32, name="edge_f32")
+            two = slice(2 * pair, 2 * pair + 2)
+            nc.vector.tensor_scalar_max(
+                out=live["deg", b][:, two].unsqueeze(2), in0=live["edge_ps", b, pair][:, :, P : P + 1], scalar1=1.0
+            )
+            nc.vector.reciprocal(out=live["recip", b][:, two], in_=live["deg", b][:, two])
+
+        def scale_edge(b, pair):
+            for i in range(2):
+                t = 2 * pair + i
+                nc.scalar.activation(
+                    out=live["edge_f32", b][:, t, :],
+                    in_=live["edge_ps", b, pair][:, i, 0:P],
+                    func=ACT.Copy,
+                    scale=live["recip", b][:, t : t + 1],
+                )
+
+        def round_edge(b, g):
+            if g == 0:
+                live["edge_in", b] = work.tile([P, PASSES, P, PACK], BF16, align_bytes=64, name="edge_in")
+                live["edge_words", b] = work.tile([P, PASSES, P], U32, align_bytes=64, name="edge_words")
+                live["edge_scales", b] = work.tile([P, PASSES, P], U8, align_bytes=64, name="edge_scales")
+            nc.gpsimd.tensor_scalar(
+                out=live["edge_in", b][:, g, :, :],
+                in0=live["edge_f32", b][:, PACK * g : PACK * (g + 1), :].rearrange("p e c -> p c e"),
+                scalar1=1.0,
+                scalar2=0.0,
+                op0=ALU.mult,
+                op1=ALU.add,
+            )
+
+        def quantise_edge(b, g):
+            nc.vector.quantize_mx(
+                out=live["edge_words", b][:, g, :].bitcast(FP8X4),
+                scales=live["edge_scales", b][:, g, :],
+                in_=live["edge_in", b][:, g, :, :].rearrange("p c e -> p (c e)"),
+            )
+
+        def vert_sums(b, g):
+            vert_ps = post_banks.tile([P, PACK, P], F32, tag="post")
+            for e in range(PACK):
+                inc_times(vert_ps[:, e, :], b, PACK * g + e, live["edge_words", b], live["edge_scales", b])
+            live["vert_ps", b, g] = vert_ps
+
+        def scale_vert(b, g):
+            vert = work.tile([P, PACK, P], F32)
+            for e in range(PACK):
+                t = PACK * g + e
+                nc.scalar.activation(
+                    out=vert[:, e, :], in_=live["vert_ps", b, g][:, e, :], func=ACT.Copy, scale=live["recip", b][:, t : t + 1]
+                )
+            live["vert", b, g] = vert
+
+        def transpose_vert(b, g):
+            vert_t_ps = post_banks.tile([P, PACK, P], F32, tag="post")
+            for e in range(PACK):
+                nc.tensor.transpose(vert_t_ps[:, e, :], live["vert", b, g][:, e, :], ident_f32[:])
+            live["vert_t_ps", b, g] = vert_t_ps
+
+        def copy_vert(b, g):
+            vert_t = work.tile([P, BANK], F32)
+            nc.scalar.copy(out=vert_t[:], in_=live["vert_t_ps", b, g][:].rearrange("p e w -> p (e w)"))
+            live["vert_t", b, g] = vert_t
+
+        def add_x_and_store(b, g):
+            half = slice(g * BANK, (g + 1) * BANK)
+            out_sb = work.tile([P, BANK], F32)
+            nc.gpsimd.tensor_tensor(out=out_sb[:], in0=live["vert_t", b, g][:], in1=x_sb[:, b, half], op=ALU.add)
+            nc.sync.dma_start(out=out[b].rearrange("c h w -> c (h w)")[:, half], in_=out_sb[:])
+
+        def stage(i, first, parts, piece, b):
+            if first <= i < first + parts and 0 <= b < BATCH:
+                piece(b, i - first)
+
+        for b in range(-1, BATCH + 1):
+            for i in range(STEPS):
+                ahead_b, ahead_i = divmod(STEPS * b + i + AHEAD, STEPS)
+                if 0 <= ahead_b < BATCH:
+                    gram_bank(ahead_b, ahead_i)
+                if 0 <= b < BATCH:
+                    compare(b, i)
+                stage(i, 0, 1, transpose_x, b + 1)
+                stage(i, 1, 2, square_sums, b + 1)
+                stage(i, 4, 1, half_thresholds, b + 1)
+                stage(i, 4, 2, repeat_h, b + 1)
+                stage(i, 6, 2, transpose_h, b + 1)
+                stage(i, 7, 2, copy_h, b + 1)
+                stage(i, 9, 2, table_first_pass, b + 1)
+                stage(i, 0, 2, table_second_pass, b)
+                stage(i, 8, 2, project, b + 1)
+                stage(i, 10, 2, round_xe, b + 1)
+                stage(i, 14, 2, quantise_xe, b + 1)
+                stage(i, 0, 4, edge_sums, b - 1)
+                stage(i, 2, 4, reciprocals, b - 1)
+                stage(i, 3, 4, scale_edge, b - 1)
+                stage(i, 6, 2, round_edge, b - 1)
+                stage(i, 8, 2, quantise_edge, b - 1)
+                stage(i, 10, 2, vert_sums, b - 1)
+                stage(i, 11, 2, scale_vert, b - 1)
+                stage(i, 12, 2, transpose_vert, b - 1)
+                stage(i, 13, 2, copy_vert, b - 1)
+                stage(i, 14, 2, add_x_and_store, b - 1)

@@ -17,9 +17,10 @@ PIXELS = 1024
 TILES = PIXELS // P
 PACK = 4
 PASSES = TILES // PACK
-BANK = 512
+HALF = PACK * P
 THRESHOLD = 16.0
-STEPS = PASSES * TILES
+QUADRANTS = ((0, 1), (0, 0), (1, 1))
+STEPS = len(QUADRANTS) * PACK
 GRAM_RING = 3
 AHEAD = GRAM_RING - 1
 
@@ -32,8 +33,7 @@ def tile_hypercomputemodule_pa_t_kernel(tc, x, W_fc, b_fc, out):
         consts = ctx.enter_context(tc.tile_pool(name="consts", bufs=1))
         small = ctx.enter_context(tc.tile_pool(name="small", bufs=2))
         work = ctx.enter_context(tc.tile_pool(name="work", bufs=2))
-        tables = ctx.enter_context(tc.tile_pool(name="tables", bufs=1))
-        incidence = ctx.enter_context(tc.tile_pool(name="incidence", bufs=2))
+        single = ctx.enter_context(tc.tile_pool(name="single", bufs=1))
         gram_banks = ctx.enter_context(tc.psum_pool(name="gram_banks", bufs=GRAM_RING))
         prep_banks = ctx.enter_context(tc.psum_pool(name="prep_banks", bufs=2))
         post_banks = ctx.enter_context(tc.psum_pool(name="post_banks", bufs=3))
@@ -59,17 +59,15 @@ def tile_hypercomputemodule_pa_t_kernel(tc, x, W_fc, b_fc, out):
         w_t = consts.tile([P, P], BF16)
         nc.vector.tensor_copy(out=w_t[:], in_=w_ps[:])
 
-        ones_in = consts.tile([P, PACK * P], BF16, align_bytes=64)
+        ones_in = consts.tile([P, PASSES * P * PACK], BF16, align_bytes=64)
         nc.vector.memset(ones_in[:], 1.0)
-        xe_words = [consts.tile([P, PASSES, 2 * P], U32, align_bytes=64, name="xe_words%d" % s) for s in range(2)]
-        xe_scales = [consts.tile([P, PASSES, 2 * P], U8, align_bytes=64, name="xe_scales%d" % s) for s in range(2)]
-        for s in range(2):
-            for g in range(PASSES):
-                nc.vector.quantize_mx(
-                    out=xe_words[s][:, g, P : 2 * P].bitcast(FP8X4),
-                    scales=xe_scales[s][:, g, P : 2 * P],
-                    in_=ones_in[:],
-                )
+        ones_words = consts.tile([P, PASSES, P], U32, align_bytes=64)
+        ones_scales = consts.tile([P, PASSES, P], U8, align_bytes=64)
+        nc.vector.quantize_mx(
+            out=ones_words[:].rearrange("p g c -> p (g c)").bitcast(FP8X4),
+            scales=ones_scales[:].rearrange("p g c -> p (g c)"),
+            in_=ones_in[:],
+        )
 
         live = {}
 
@@ -93,8 +91,8 @@ def tile_hypercomputemodule_pa_t_kernel(tc, x, W_fc, b_fc, out):
                     accum_out=live["sq", b][:, t : t + 1],
                 )
 
-        def half_thresholds(b, part):
-            h_col = small.tile([P, TILES], F32)
+        def h_columns(b, part):
+            h_col = small.tile([P, TILES], F32, bufs=3)
             nc.vector.tensor_scalar(
                 out=h_col[:],
                 in0=live["sq", b][:],
@@ -104,54 +102,40 @@ def tile_hypercomputemodule_pa_t_kernel(tc, x, W_fc, b_fc, out):
                 op1=ALU.add,
             )
             live["h_col", b] = h_col
-            live["h_rep", b] = work.tile([P, TILES, P], F32, name="h_rep")
             live["h_row", b] = work.tile([P, PIXELS], F32, name="h_row")
 
-        def repeat_h(b, g):
-            tiles_of_pass = slice(PACK * g, PACK * (g + 1))
-            nc.gpsimd.tensor_scalar(
-                out=live["h_rep", b][:, tiles_of_pass, :],
-                in0=live["h_col", b][:, tiles_of_pass].unsqueeze(2).to_broadcast([P, PACK, P]),
-                scalar1=1.0,
-                scalar2=0.0,
-                op0=ALU.mult,
-                op1=ALU.add,
-            )
-
-        def transpose_h(b, g):
+        def spread_h(b, g):
             h_ps = prep_banks.tile([P, PACK, P], F32, tag="prep")
             for e in range(PACK):
-                nc.tensor.transpose(h_ps[:, e, :], live["h_rep", b][:, PACK * g + e, :], ident_f32[:])
+                t = PACK * g + e
+                nc.tensor.transpose(h_ps[:, e, :], live["h_col", b][:, t : t + 1].to_broadcast([P, P]), ident_f32[:])
             live["h_ps", b, g] = h_ps
 
         def copy_h(b, g):
             nc.scalar.copy(
-                out=live["h_row", b][:, g * BANK : (g + 1) * BANK], in_=live["h_ps", b, g][:].rearrange("p e w -> p (e w)")
+                out=live["h_row", b][:, g * HALF : (g + 1) * HALF], in_=live["h_ps", b, g][:].rearrange("p e w -> p (e w)")
             )
 
-        def table_rows(b, g, pair):
-            if pair == 0:
-                live["thresh", b, g] = tables.tile([P, PACK, PIXELS], F32, tag="thresh%d" % g, name="thresh")
-            thresh = live["thresh", b, g]
-            e = 2 * pair
-            t = PACK * g + e
-            nc.scalar.activation(
-                out=thresh[:, e, :], in_=live["h_row", b][:], func=ACT.Identity, bias=live["h_col", b][:, t : t + 1]
-            )
-            nc.gpsimd.tensor_scalar(
-                out=thresh[:, e + 1, :],
-                in0=live["h_row", b][:],
-                scalar1=1.0,
-                scalar2=live["h_col", b][:, t + 1 : t + 2],
-                op0=ALU.mult,
-                op1=ALU.add,
-            )
+        def table_row(b, q, e):
+            g, c = QUADRANTS[q]
+            if e == 0:
+                live["thresh", b, q] = single.tile([P, PACK, HALF], F32, tag="thresh%d" % q, name="thresh")
+            row = live["thresh", b, q][:, e, :]
+            h_row = live["h_row", b][:, c * HALF : (c + 1) * HALF]
+            h_here = live["h_col", b][:, PACK * g + e : PACK * g + e + 1]
+            if e == 0:
+                nc.scalar.activation(out=row, in_=h_row, func=ACT.Identity, bias=h_here)
+            else:
+                nc.gpsimd.tensor_scalar(out=row, in0=h_row, scalar1=1.0, scalar2=h_here, op0=ALU.mult, op1=ALU.add)
 
-        def table_first_pass(b, pair):
-            table_rows(b, 0, pair)
+        def table_0(b, e):
+            table_row(b, 0, e)
 
-        def table_second_pass(b, pair):
-            table_rows(b, 1, pair)
+        def table_1(b, e):
+            table_row(b, 1, e)
+
+        def table_2(b, e):
+            table_row(b, 2, e)
 
         def project(b, g):
             xe_ps = prep_banks.tile([P, PACK, P], F32, tag="prep")
@@ -161,114 +145,132 @@ def tile_hypercomputemodule_pa_t_kernel(tc, x, W_fc, b_fc, out):
             live["xe_ps", b, g] = xe_ps
 
         def round_xe(b, g):
-            xe_in = work.tile([P, P, PACK], BF16, align_bytes=64)
-            nc.scalar.copy(out=xe_in[:], in_=live["xe_ps", b, g][:].rearrange("p e c -> p c e"))
-            live["xe_in", b, g] = xe_in
+            if g == 0:
+                live["xe_in", b] = work.tile([P, PASSES, P, PACK], BF16, align_bytes=64, name="xe_in")
+            nc.scalar.copy(out=live["xe_in", b][:, g, :, :], in_=live["xe_ps", b, g][:].rearrange("p e c -> p c e"))
 
-        def quantise_xe(b, g):
+        def quantise(b, name):
+            words = work.tile([P, PASSES, P], U32, align_bytes=64, name=name + "_words")
+            scales = work.tile([P, PASSES, P], U8, align_bytes=64, name=name + "_scales")
             nc.vector.quantize_mx(
-                out=xe_words[b % 2][:, g, 0:P].bitcast(FP8X4),
-                scales=xe_scales[b % 2][:, g, 0:P],
-                in_=live["xe_in", b, g][:].rearrange("p c e -> p (c e)"),
+                out=words[:].rearrange("p g c -> p (g c)").bitcast(FP8X4),
+                scales=scales[:].rearrange("p g c -> p (g c)"),
+                in_=live[name + "_in", b][:].rearrange("p g c e -> p (g c e)"),
             )
+            live[name + "_words", b] = words
+            live[name + "_scales", b] = scales
+
+        def quantise_xe(b, part):
+            quantise(b, "xe")
 
         def gram_bank(b, i):
-            g, nb = divmod(i, TILES)
+            q, j = divmod(i, PACK)
+            g, c = QUADRANTS[q]
             gram = gram_banks.tile([P, PACK, P], F32)
             for e in range(PACK):
                 nc.tensor.matmul(
-                    gram[:, e, :], lhsT=pixel_tile(b, PACK * g + e), rhs=pixel_tile(b, nb), start=True, stop=True
+                    gram[:, e, :], lhsT=pixel_tile(b, PACK * g + e), rhs=pixel_tile(b, PACK * c + j), start=True, stop=True
                 )
             live["gram", b, i] = gram
 
         def compare(b, i):
-            g, nb = divmod(i, TILES)
-            cols = slice(nb * P, (nb + 1) * P)
+            q, j = divmod(i, PACK)
+            g, c = QUADRANTS[q]
             if i == 0:
-                live["inc_words", b] = incidence.tile([P, PASSES, PIXELS], U32, align_bytes=64, name="inc_words")
-                live["inc_scales", b] = incidence.tile([P, PASSES, PIXELS], U8, align_bytes=64, name="inc_scales")
-            if nb == 0:
-                live["inc_in", b] = incidence.tile([P, PIXELS, PACK], BF16, align_bytes=64, name="inc_in")
-            inc_in = live["inc_in", b]
+                for s in range(PASSES):
+                    live["inc_in", b, s] = single.tile(
+                        [P, PIXELS, PACK], BF16, align_bytes=64, tag="inc_in%d" % s, name="inc_in"
+                    )
+            first = (PACK * c + j) * P
             nc.vector.tensor_tensor(
-                out=inc_in[:, cols, :],
+                out=live["inc_in", b, g][:, first : first + P, :],
                 in0=live["gram", b, i][:].rearrange("p e w -> p w e"),
-                in1=live["thresh", b, g][:, :, cols].rearrange("p e w -> p w e"),
+                in1=live["thresh", b, q][:, :, j * P : (j + 1) * P].rearrange("p e w -> p w e"),
                 op=ALU.is_gt,
             )
-            if nb == TILES - 1:
-                nc.vector.quantize_mx(
-                    out=live["inc_words", b][:, g, :].bitcast(FP8X4),
-                    scales=live["inc_scales", b][:, g, :],
-                    in_=inc_in[:].rearrange("p w e -> p (w e)"),
-                )
 
-        def inc_times(acc, b, t, rhs_words, rhs_scales):
-            cols = slice(t * P, (t + 1) * P)
-            for g in range(PASSES):
-                nc.tensor.matmul_mx(
-                    out=acc,
-                    lhsT=live["inc_words", b][:, g, cols].bitcast(FP8X4),
-                    lhsT_scale=live["inc_scales", b][:, g, cols],
-                    rhs=rhs_words[:, g, :].bitcast(FP8X4),
-                    rhs_scale=rhs_scales[:, g, :],
-                    start=(g == 0),
-                    stop=(g == PASSES - 1),
-                )
+        def mirror(b, pair):
+            mirror_ps = prep_banks.tile([P, 2, PACK, P], BF16, tag="prep")
+            for a in range(2):
+                for e in range(PACK):
+                    first = HALF + e * P
+                    nc.tensor.transpose(
+                        mirror_ps[:, a, e, :], live["inc_in", b, 0][:, first : first + P, 2 * pair + a], ident_bf[:]
+                    )
+            live["mirror_ps", b, pair] = mirror_ps
 
-        def edge_sums(b, pair):
-            edge_ps = post_banks.tile([P, 2, 2 * P], F32, tag="post")
-            for i in range(2):
-                inc_times(edge_ps[:, i, :], b, 2 * pair + i, xe_words[b % 2], xe_scales[b % 2])
-            live["edge_ps", b, pair] = edge_ps
-
-        def reciprocals(b, pair):
-            if pair == 0:
-                live["deg", b] = small.tile([P, TILES], F32, name="deg")
-                live["recip", b] = small.tile([P, TILES], F32, name="recip")
-                live["edge_f32", b] = work.tile([P, TILES, P], F32, name="edge_f32")
-            two = slice(2 * pair, 2 * pair + 2)
-            nc.vector.tensor_scalar_max(
-                out=live["deg", b][:, two].unsqueeze(2), in0=live["edge_ps", b, pair][:, :, P : P + 1], scalar1=1.0
+        def copy_mirror(b, pair):
+            nc.scalar.copy(
+                out=live["inc_in", b, 1][:, 2 * pair * P : 2 * (pair + 1) * P, :].rearrange("p (a w) e -> p a w e", a=2),
+                in_=live["mirror_ps", b, pair][:].rearrange("p a e w -> p a w e"),
             )
-            nc.vector.reciprocal(out=live["recip", b][:, two], in_=live["deg", b][:, two])
 
-        def scale_edge(b, pair):
-            for i in range(2):
-                t = 2 * pair + i
-                nc.scalar.activation(
-                    out=live["edge_f32", b][:, t, :],
-                    in_=live["edge_ps", b, pair][:, i, 0:P],
-                    func=ACT.Copy,
-                    scale=live["recip", b][:, t : t + 1],
-                )
+        def quantise_inc(b, g):
+            if g == 0:
+                live["inc_words", b] = work.tile([P, PASSES, PIXELS], U32, align_bytes=64, name="inc_words")
+                live["inc_scales", b] = work.tile([P, PASSES, PIXELS], U8, align_bytes=64, name="inc_scales")
+            nc.vector.quantize_mx(
+                out=live["inc_words", b][:, g, :].bitcast(FP8X4),
+                scales=live["inc_scales", b][:, g, :],
+                in_=live["inc_in", b, g][:].rearrange("p w e -> p (w e)"),
+            )
+
+        def quantise_first_pass(b, part):
+            quantise_inc(b, 0)
+
+        def quantise_second_pass(b, part):
+            quantise_inc(b, 1)
+
+        def inc_times(b, g, rhs_words, rhs_scales):
+            bank = post_banks.tile([P, PACK, P], F32, tag="post")
+            for e in range(PACK):
+                cols = slice((PACK * g + e) * P, (PACK * g + e + 1) * P)
+                for s in range(PASSES):
+                    nc.tensor.matmul_mx(
+                        out=bank[:, e, :],
+                        lhsT=live["inc_words", b][:, s, cols].bitcast(FP8X4),
+                        lhsT_scale=live["inc_scales", b][:, s, cols],
+                        rhs=rhs_words[:, s, :].bitcast(FP8X4),
+                        rhs_scale=rhs_scales[:, s, :],
+                        start=(s == 0),
+                        stop=(s == PASSES - 1),
+                    )
+            return bank
+
+        def degree_sums(b, g):
+            live["deg_ps", b, g] = inc_times(b, g, ones_words, ones_scales)
+
+        def reciprocals(b, g):
+            if g == 0:
+                live["deg", b] = small.tile([P, TILES], F32, name="deg")
+            nc.vector.tensor_scalar_max(
+                out=live["deg", b][:, PACK * g : PACK * (g + 1)].unsqueeze(2),
+                in0=live["deg_ps", b, g][:, :, 0:1],
+                scalar1=1.0,
+            )
+            if g == PASSES - 1:
+                recip = small.tile([P, TILES], F32, bufs=3)
+                nc.vector.reciprocal(out=recip[:], in_=live["deg", b][:])
+                live["recip", b] = recip
+
+        def edge_sums(b, g):
+            live["edge_ps", b, g] = inc_times(b, g, live["xe_words", b], live["xe_scales", b])
 
         def round_edge(b, g):
             if g == 0:
                 live["edge_in", b] = work.tile([P, PASSES, P, PACK], BF16, align_bytes=64, name="edge_in")
-                live["edge_words", b] = work.tile([P, PASSES, P], U32, align_bytes=64, name="edge_words")
-                live["edge_scales", b] = work.tile([P, PASSES, P], U8, align_bytes=64, name="edge_scales")
-            nc.gpsimd.tensor_scalar(
+            nc.vector.tensor_tensor(
                 out=live["edge_in", b][:, g, :, :],
-                in0=live["edge_f32", b][:, PACK * g : PACK * (g + 1), :].rearrange("p e c -> p c e"),
-                scalar1=1.0,
-                scalar2=0.0,
-                op0=ALU.mult,
-                op1=ALU.add,
+                in0=live["edge_ps", b, g][:].rearrange("p e c -> p c e"),
+                in1=live["recip", b][:, PACK * g : PACK * (g + 1)].unsqueeze(1).to_broadcast([P, P, PACK]),
+                op=ALU.mult,
             )
 
-        def quantise_edge(b, g):
-            nc.vector.quantize_mx(
-                out=live["edge_words", b][:, g, :].bitcast(FP8X4),
-                scales=live["edge_scales", b][:, g, :],
-                in_=live["edge_in", b][:, g, :, :].rearrange("p c e -> p (c e)"),
-            )
+        def quantise_edge(b, part):
+            quantise(b, "edge")
 
         def vert_sums(b, g):
-            vert_ps = post_banks.tile([P, PACK, P], F32, tag="post")
-            for e in range(PACK):
-                inc_times(vert_ps[:, e, :], b, PACK * g + e, live["edge_words", b], live["edge_scales", b])
-            live["vert_ps", b, g] = vert_ps
+            live["vert_ps", b, g] = inc_times(b, g, live["edge_words", b], live["edge_scales", b])
 
         def scale_vert(b, g):
             vert = work.tile([P, PACK, P], F32)
@@ -279,52 +281,52 @@ def tile_hypercomputemodule_pa_t_kernel(tc, x, W_fc, b_fc, out):
                 )
             live["vert", b, g] = vert
 
-        def transpose_vert(b, g):
-            vert_t_ps = post_banks.tile([P, PACK, P], F32, tag="post")
+        def add_x(b, g):
+            out_ps = post_banks.tile([P, PACK, P], F32, tag="post")
             for e in range(PACK):
-                nc.tensor.transpose(vert_t_ps[:, e, :], live["vert", b, g][:, e, :], ident_f32[:])
-            live["vert_t_ps", b, g] = vert_t_ps
+                nc.tensor.matmul(out_ps[:, e, :], lhsT=ident_bf[:], rhs=pixel_tile(b, PACK * g + e), start=True, stop=False)
+                nc.tensor.matmul(
+                    out_ps[:, e, :], lhsT=live["vert", b, g][:, e, :], rhs=ident_f32[:], is_transpose=True, start=False, stop=True
+                )
+            live["out_ps", b, g] = out_ps
 
-        def copy_vert(b, g):
-            vert_t = work.tile([P, BANK], F32)
-            nc.scalar.copy(out=vert_t[:], in_=live["vert_t_ps", b, g][:].rearrange("p e w -> p (e w)"))
-            live["vert_t", b, g] = vert_t
-
-        def add_x_and_store(b, g):
-            half = slice(g * BANK, (g + 1) * BANK)
-            out_sb = work.tile([P, BANK], F32)
-            nc.gpsimd.tensor_tensor(out=out_sb[:], in0=live["vert_t", b, g][:], in1=x_sb[:, b, half], op=ALU.add)
-            nc.sync.dma_start(out=out[b].rearrange("c h w -> c (h w)")[:, half], in_=out_sb[:])
+        def store(b, g):
+            out_sb = work.tile([P, HALF], F32)
+            nc.scalar.copy(out=out_sb[:], in_=live["out_ps", b, g][:].rearrange("p e w -> p (e w)"))
+            nc.sync.dma_start(out=out[b].rearrange("c h w -> c (h w)")[:, g * HALF : (g + 1) * HALF], in_=out_sb[:])
 
         def stage(i, first, parts, piece, b):
             if first <= i < first + parts and 0 <= b < BATCH:
                 piece(b, i - first)
 
-        for b in range(-1, BATCH + 1):
+        for b in range(-2, BATCH + 2):
             for i in range(STEPS):
                 ahead_b, ahead_i = divmod(STEPS * b + i + AHEAD, STEPS)
                 if 0 <= ahead_b < BATCH:
                     gram_bank(ahead_b, ahead_i)
                 if 0 <= b < BATCH:
                     compare(b, i)
-                stage(i, 0, 1, transpose_x, b + 1)
-                stage(i, 1, 2, square_sums, b + 1)
-                stage(i, 4, 1, half_thresholds, b + 1)
-                stage(i, 4, 2, repeat_h, b + 1)
-                stage(i, 6, 2, transpose_h, b + 1)
-                stage(i, 7, 2, copy_h, b + 1)
-                stage(i, 9, 2, table_first_pass, b + 1)
-                stage(i, 0, 2, table_second_pass, b)
-                stage(i, 8, 2, project, b + 1)
-                stage(i, 10, 2, round_xe, b + 1)
-                stage(i, 14, 2, quantise_xe, b + 1)
-                stage(i, 0, 4, edge_sums, b - 1)
-                stage(i, 2, 4, reciprocals, b - 1)
-                stage(i, 3, 4, scale_edge, b - 1)
-                stage(i, 6, 2, round_edge, b - 1)
-                stage(i, 8, 2, quantise_edge, b - 1)
-                stage(i, 10, 2, vert_sums, b - 1)
-                stage(i, 11, 2, scale_vert, b - 1)
-                stage(i, 12, 2, transpose_vert, b - 1)
-                stage(i, 13, 2, copy_vert, b - 1)
-                stage(i, 14, 2, add_x_and_store, b - 1)
+                stage(i, 0, PACK, table_2, b)
+                stage(i, 4, PACK, table_0, b + 1)
+                stage(i, 8, PACK, table_1, b + 1)
+                stage(i, 0, 1, transpose_x, b + 2)
+                stage(i, 1, 2, square_sums, b + 2)
+                stage(i, 5, 1, h_columns, b + 2)
+                stage(i, 9, 2, spread_h, b + 2)
+                stage(i, 10, 2, copy_h, b + 2)
+                stage(i, 3, 2, project, b + 1)
+                stage(i, 4, 2, round_xe, b + 1)
+                stage(i, 8, 1, quantise_xe, b + 1)
+                stage(i, 6, 2, mirror, b)
+                stage(i, 7, 2, copy_mirror, b)
+                stage(i, 0, 2, vert_sums, b - 2)
+                stage(i, 1, 2, scale_vert, b - 2)
+                stage(i, 8, 2, add_x, b - 2)
+                stage(i, 9, 2, store, b - 2)
+                stage(i, 2, 2, degree_sums, b - 1)
+                stage(i, 5, 2, reciprocals, b - 1)
+                stage(i, 5, 2, edge_sums, b - 1)
+                stage(i, 8, 2, round_edge, b - 1)
+                stage(i, 9, 1, quantise_edge, b - 1)
+                stage(i, 8, 1, quantise_first_pass, b)
+                stage(i, 11, 1, quantise_second_pass, b)

@@ -19,6 +19,7 @@ PACK = 4
 PASSES = TILES // PACK
 HALF = PACK * P
 THRESHOLD = 16.0
+RUN = 4
 QUADRANTS = ((0, 1), (0, 0), (1, 1))
 STEPS = len(QUADRANTS) * PACK
 GRAM_RING = 3
@@ -183,9 +184,9 @@ def tile_hypercomputemodule_pa_t_kernel(tc, x, W_fc, b_fc, out):
                     )
             first = (PACK * c + j) * P
             nc.vector.tensor_tensor(
-                out=live["inc_in", b, g][:, first : first + P, :],
-                in0=live["gram", b, i][:].rearrange("p e w -> p w e"),
-                in1=live["thresh", b, q][:, :, j * P : (j + 1) * P].rearrange("p e w -> p w e"),
+                out=live["inc_in", b, g][:, first : first + P, :].rearrange("p (r i) e -> p r e i", i=RUN),
+                in0=live["gram", b, i][:].rearrange("p e (r i) -> p r e i", i=RUN),
+                in1=live["thresh", b, q][:, :, j * P : (j + 1) * P].rearrange("p e (r i) -> p r e i", i=RUN),
                 op=ALU.is_gt,
             )
 
@@ -260,9 +261,9 @@ def tile_hypercomputemodule_pa_t_kernel(tc, x, W_fc, b_fc, out):
             if g == 0:
                 live["edge_in", b] = work.tile([P, PASSES, P, PACK], BF16, align_bytes=64, name="edge_in")
             nc.vector.tensor_tensor(
-                out=live["edge_in", b][:, g, :, :],
-                in0=live["edge_ps", b, g][:].rearrange("p e c -> p c e"),
-                in1=live["recip", b][:, PACK * g : PACK * (g + 1)].unsqueeze(1).to_broadcast([P, P, PACK]),
+                out=live["edge_in", b][:, g, :, :].rearrange("p (r i) e -> p r e i", i=RUN),
+                in0=live["edge_ps", b, g][:].rearrange("p e (r i) -> p r e i", i=RUN),
+                in1=live["recip", b][:, PACK * g : PACK * (g + 1)].unsqueeze(1).unsqueeze(3).to_broadcast([P, P // RUN, PACK, RUN]),
                 op=ALU.mult,
             )
 

@@ -94,13 +94,8 @@ def tile_hypercomputemodule_pa_t_kernel(tc, x, W_fc, b_fc, out):
 
         def h_columns(b, part):
             h_col = small.tile([P, TILES], F32, bufs=3)
-            nc.vector.tensor_scalar(
-                out=h_col[:],
-                in0=live["sq", b][:],
-                scalar1=0.5,
-                scalar2=-THRESHOLD * THRESHOLD / 4.0,
-                op0=ALU.mult,
-                op1=ALU.add,
+            nc.scalar.activation(
+                out=h_col[:], in_=live["sq", b][:], func=ACT.Copy, scale=0.5, bias=-THRESHOLD * THRESHOLD / 4.0
             )
             live["h_col", b] = h_col
             live["h_row", b] = work.tile([P, PIXELS], F32, name="h_row")
@@ -312,22 +307,22 @@ def tile_hypercomputemodule_pa_t_kernel(tc, x, W_fc, b_fc, out):
                 stage(i, 8, PACK, table_1, b + 1)
                 stage(i, 0, 1, transpose_x, b + 2)
                 stage(i, 1, 2, square_sums, b + 2)
-                stage(i, 5, 1, h_columns, b + 2)
+                stage(i, 3, 1, h_columns, b + 2)
                 stage(i, 9, 2, spread_h, b + 2)
                 stage(i, 10, 2, copy_h, b + 2)
                 stage(i, 3, 2, project, b + 1)
                 stage(i, 4, 2, round_xe, b + 1)
-                stage(i, 8, 1, quantise_xe, b + 1)
                 stage(i, 6, 2, mirror, b)
                 stage(i, 7, 2, copy_mirror, b)
-                stage(i, 0, 2, vert_sums, b - 2)
-                stage(i, 1, 2, scale_vert, b - 2)
+                stage(i, 1, 2, vert_sums, b - 2)
+                stage(i, 2, 2, scale_vert, b - 2)
                 stage(i, 8, 2, add_x, b - 2)
                 stage(i, 9, 2, store, b - 2)
                 stage(i, 2, 2, degree_sums, b - 1)
                 stage(i, 5, 2, reciprocals, b - 1)
                 stage(i, 5, 2, edge_sums, b - 1)
                 stage(i, 8, 2, round_edge, b - 1)
-                stage(i, 9, 1, quantise_edge, b - 1)
-                stage(i, 8, 1, quantise_first_pass, b)
+                stage(i, 10, 1, quantise_edge, b - 1)
+                stage(i, 7, 1, quantise_first_pass, b)
+                stage(i, 7, 1, quantise_xe, b + 1)
                 stage(i, 11, 1, quantise_second_pass, b)

@@ -32,12 +32,11 @@ def tile_hypercomputemodule_pa_t_kernel(tc, x, W_fc, b_fc, out):
     nc = tc.nc
     with ExitStack() as ctx:
         consts = ctx.enter_context(tc.tile_pool(name="consts", bufs=1))
-        small = ctx.enter_context(tc.tile_pool(name="small", bufs=2))
+        small = ctx.enter_context(tc.tile_pool(name="small", bufs=3))
         work = ctx.enter_context(tc.tile_pool(name="work", bufs=2))
         single = ctx.enter_context(tc.tile_pool(name="single", bufs=1))
         gram_banks = ctx.enter_context(tc.psum_pool(name="gram_banks", bufs=GRAM_RING))
-        prep_banks = ctx.enter_context(tc.psum_pool(name="prep_banks", bufs=2))
-        post_banks = ctx.enter_context(tc.psum_pool(name="post_banks", bufs=3))
+        banks = ctx.enter_context(tc.psum_pool(name="banks", bufs=8 - GRAM_RING))
         ctx.enter_context(tc.manual_schedule())
 
         x_sb = consts.tile([P, BATCH, PIXELS], BF16)
@@ -50,15 +49,12 @@ def tile_hypercomputemodule_pa_t_kernel(tc, x, W_fc, b_fc, out):
         nc.scalar.dma_start(out=bias_rows[0:1, :], in_=b_fc.rearrange("(o c) -> o c", o=1))
         ones_bf = consts.tile([P, P], BF16)
         nc.vector.memset(ones_bf[:], 1.0)
+        warm = consts.tile([P, 1], F32)
+        nc.scalar.activation(out=warm[:], in_=ones_bf[:, 0:1], func=ACT.Square)
         ident_bf = consts.tile([P, P], BF16)
         make_identity(nc, ident_bf[:])
         ident_f32 = consts.tile([P, P], F32)
         make_identity(nc, ident_f32[:])
-
-        w_ps = prep_banks.tile([P, P], BF16, tag="prep")
-        nc.tensor.transpose(w_ps[:], w_sb[:], ident_bf[:])
-        w_t = consts.tile([P, P], BF16)
-        nc.vector.tensor_copy(out=w_t[:], in_=w_ps[:])
 
         ones_in = consts.tile([P, PASSES * P * PACK], BF16, align_bytes=64)
         nc.vector.memset(ones_in[:], 1.0)
@@ -69,72 +65,60 @@ def tile_hypercomputemodule_pa_t_kernel(tc, x, W_fc, b_fc, out):
             scales=ones_scales[:].rearrange("p g c -> p (g c)"),
             in_=ones_in[:],
         )
+        w_t = consts.tile([P, P], BF16)
 
         live = {}
 
         def pixel_tile(b, t):
             return x_sb[:, b, t * P : (t + 1) * P]
 
-        def transpose_x(b, part):
-            xf_ps = prep_banks.tile([P, TILES, P], BF16, tag="prep")
-            for t in range(TILES):
-                nc.tensor.transpose(xf_ps[:, t, :], pixel_tile(b, t), ident_bf[:])
-            live["xf_ps", b] = xf_ps
-            live["squares", b] = work.tile([P, TILES, P], BF16, name="squares")
-            live["sq", b] = small.tile([P, TILES], F32, name="sq")
+        def transpose_w(b, part):
+            w_ps = banks.tile([P, P], BF16, tag="bank")
+            nc.tensor.transpose(w_ps[:], w_sb[:], ident_bf[:])
+            nc.vector.tensor_copy(out=w_t[:], in_=w_ps[:])
 
-        def square_sums(b, g):
-            for t in range(PACK * g, PACK * (g + 1)):
+        def transpose_x(b, part):
+            g = 1 - part
+            xf_ps = banks.tile([P, PACK, P], BF16, tag="bank")
+            for e in range(PACK):
+                nc.tensor.transpose(xf_ps[:, e, :], pixel_tile(b, PACK * g + e), ident_bf[:])
+            live["xf_ps", b, g] = xf_ps
+            if part == 0:
+                live["squares", b] = work.tile([P, TILES, P], BF16, name="squares")
+                live["sq", b] = small.tile([P, TILES], F32, name="sq")
+                live["h_col", b] = small.tile([P, TILES], F32, name="h_col")
+                live["h_row", b] = work.tile([P, PIXELS], F32, name="h_row")
+
+        def square_sums(b, part):
+            g = 1 - part
+            for e in range(PACK):
+                t = PACK * g + e
                 nc.scalar.activation(
-                    out=live["squares", b][:, t, :],
-                    in_=live["xf_ps", b][:, t, :],
-                    func=ACT.Square,
+                    out=live["squares", b][:, t, :], in_=live["xf_ps", b, g][:, e, :], func=ACT.Square,
                     accum_out=live["sq", b][:, t : t + 1],
                 )
-
-        def h_columns(b, part):
-            h_col = small.tile([P, TILES], F32, bufs=3)
+            cols = slice(PACK * g, PACK * (g + 1))
             nc.scalar.activation(
-                out=h_col[:], in_=live["sq", b][:], func=ACT.Copy, scale=0.5, bias=-THRESHOLD * THRESHOLD / 4.0
+                out=live["h_col", b][:, cols], in_=live["sq", b][:, cols], func=ACT.Copy, scale=0.5,
+                bias=-THRESHOLD * THRESHOLD / 4.0,
             )
-            live["h_col", b] = h_col
-            live["h_row", b] = work.tile([P, PIXELS], F32, name="h_row")
 
-        def spread_h(b, g):
-            h_ps = prep_banks.tile([P, PACK, P], F32, tag="prep")
+        def spread_h(b, part):
+            g = 1 - part
+            h_ps = banks.tile([P, PACK, P], F32, tag="bank")
             for e in range(PACK):
                 t = PACK * g + e
                 nc.tensor.transpose(h_ps[:, e, :], live["h_col", b][:, t : t + 1].to_broadcast([P, P]), ident_f32[:])
             live["h_ps", b, g] = h_ps
 
-        def copy_h(b, g):
+        def copy_h(b, part):
+            g = 1 - part
             nc.scalar.copy(
                 out=live["h_row", b][:, g * HALF : (g + 1) * HALF], in_=live["h_ps", b, g][:].rearrange("p e w -> p (e w)")
             )
 
-        def table_row(b, q, e):
-            g, c = QUADRANTS[q]
-            if e == 0:
-                live["thresh", b, q] = single.tile([P, PACK, HALF], F32, tag="thresh%d" % q, name="thresh")
-            row = live["thresh", b, q][:, e, :]
-            h_row = live["h_row", b][:, c * HALF : (c + 1) * HALF]
-            h_here = live["h_col", b][:, PACK * g + e : PACK * g + e + 1]
-            if e == 0:
-                nc.scalar.activation(out=row, in_=h_row, func=ACT.Identity, bias=h_here)
-            else:
-                nc.gpsimd.tensor_scalar(out=row, in0=h_row, scalar1=1.0, scalar2=h_here, op0=ALU.mult, op1=ALU.add)
-
-        def table_0(b, e):
-            table_row(b, 0, e)
-
-        def table_1(b, e):
-            table_row(b, 1, e)
-
-        def table_2(b, e):
-            table_row(b, 2, e)
-
         def project(b, g):
-            xe_ps = prep_banks.tile([P, PACK, P], F32, tag="prep")
+            xe_ps = banks.tile([P, PACK, P], F32, tag="bank")
             for e in range(PACK):
                 nc.tensor.matmul(xe_ps[:, e, :], lhsT=ones_bf[:], rhs=bias_rows[:], start=True, stop=False)
                 nc.tensor.matmul(xe_ps[:, e, :], lhsT=pixel_tile(b, PACK * g + e), rhs=w_t[:], start=False, stop=True)
@@ -146,8 +130,8 @@ def tile_hypercomputemodule_pa_t_kernel(tc, x, W_fc, b_fc, out):
             nc.scalar.copy(out=live["xe_in", b][:, g, :, :], in_=live["xe_ps", b, g][:].rearrange("p e c -> p c e"))
 
         def quantise(b, name):
-            words = work.tile([P, PASSES, P], U32, align_bytes=64, name=name + "_words")
-            scales = work.tile([P, PASSES, P], U8, align_bytes=64, name=name + "_scales")
+            words = work.tile([P, PASSES, P], U32, align_bytes=64, name=name + "_words", bufs=3)
+            scales = work.tile([P, PASSES, P], U8, align_bytes=64, name=name + "_scales", bufs=3)
             nc.vector.quantize_mx(
                 out=words[:].rearrange("p g c -> p (g c)").bitcast(FP8X4),
                 scales=scales[:].rearrange("p g c -> p (g c)"),
@@ -160,76 +144,89 @@ def tile_hypercomputemodule_pa_t_kernel(tc, x, W_fc, b_fc, out):
             quantise(b, "xe")
 
         def gram_bank(b, i):
-            q, j = divmod(i, PACK)
+            q, e = divmod(i, PACK)
             g, c = QUADRANTS[q]
-            gram = gram_banks.tile([P, PACK, P], F32)
-            for e in range(PACK):
-                nc.tensor.matmul(
-                    gram[:, e, :], lhsT=pixel_tile(b, PACK * g + e), rhs=pixel_tile(b, PACK * c + j), start=True, stop=True
-                )
+            gram = gram_banks.tile([P, HALF], F32)
+            nc.tensor.matmul(gram[:], lhsT=pixel_tile(b, PACK * g + e), rhs=x_sb[:, b, c * HALF : (c + 1) * HALF], start=True, stop=True)
             live["gram", b, i] = gram
 
         def compare(b, i):
-            q, j = divmod(i, PACK)
+            q, e = divmod(i, PACK)
             g, c = QUADRANTS[q]
-            if i == 0:
-                for s in range(PASSES):
-                    live["inc_in", b, s] = single.tile(
-                        [P, PIXELS, PACK], BF16, align_bytes=64, tag="inc_in%d" % s, name="inc_in"
-                    )
-            first = (PACK * c + j) * P
-            nc.vector.tensor_tensor(
-                out=live["inc_in", b, g][:, first : first + P, :].rearrange("p (r i) e -> p r e i", i=RUN),
-                in0=live["gram", b, i][:].rearrange("p e (r i) -> p r e i", i=RUN),
-                in1=live["thresh", b, q][:, :, j * P : (j + 1) * P].rearrange("p e (r i) -> p r e i", i=RUN),
-                op=ALU.is_gt,
+            if e == 0:
+                live["raw", b, q] = single.tile([P, PACK, HALF], BF16, tag="raw%d" % q, name="raw")
+            t = PACK * g + e
+            nc.vector.scalar_tensor_tensor(
+                out=live["raw", b, q][:, e, :], in0=live["gram", b, i][:], scalar=live["h_col", b][:, t : t + 1],
+                in1=live["h_row", b][:, c * HALF : (c + 1) * HALF], op0=ALU.subtract, op1=ALU.is_gt,
             )
 
         def mirror(b, pair):
-            mirror_ps = prep_banks.tile([P, 2, PACK, P], BF16, tag="prep")
+            mirror_ps = banks.tile([P, 2, PACK, P], BF16, tag="bank")
             for a in range(2):
                 for e in range(PACK):
-                    first = HALF + e * P
-                    nc.tensor.transpose(
-                        mirror_ps[:, a, e, :], live["inc_in", b, 0][:, first : first + P, 2 * pair + a], ident_bf[:]
-                    )
+                    nc.tensor.transpose(mirror_ps[:, a, e, :], live["raw", b, 0][:, 2 * pair + a, e * P : (e + 1) * P], ident_bf[:])
             live["mirror_ps", b, pair] = mirror_ps
 
         def copy_mirror(b, pair):
+            if pair == 0:
+                live["stage", b, 3] = single.tile([P, HALF, PACK], BF16, align_bytes=64, tag="stage_m", name="stage_m")
             nc.scalar.copy(
-                out=live["inc_in", b, 1][:, 2 * pair * P : 2 * (pair + 1) * P, :].rearrange("p (a w) e -> p a w e", a=2),
+                out=live["stage", b, 3][:, 2 * pair * P : 2 * (pair + 1) * P, :].rearrange("p (a w) e -> p a w e", a=2),
                 in_=live["mirror_ps", b, pair][:].rearrange("p a e w -> p a w e"),
             )
 
-        def quantise_inc(b, g):
-            if g == 0:
-                live["inc_words", b] = work.tile([P, PASSES, PIXELS], U32, align_bytes=64, name="inc_words")
-                live["inc_scales", b] = work.tile([P, PASSES, PIXELS], U8, align_bytes=64, name="inc_scales")
+        def interleave(b, q, j):
+            if j == 0:
+                live["stage", b, q] = single.tile([P, HALF, PACK], BF16, align_bytes=64, tag="stage", name="stage")
+            dst = live["stage", b, q][:, j * P : (j + 1) * P, :]
+            src = live["raw", b, q][:, :, j * P : (j + 1) * P].rearrange("p e w -> p w e")
+            if j == 0:
+                nc.scalar.copy(out=dst, in_=src)
+            else:
+                nc.gpsimd.tensor_scalar(out=dst, in0=src, scalar1=1.0, scalar2=0.0, op0=ALU.mult, op1=ALU.add)
+
+        def interleave_0(b, j):
+            interleave(b, 0, j)
+
+        def interleave_1(b, j):
+            interleave(b, 1, j)
+
+        def interleave_2(b, j):
+            interleave(b, 2, j)
+
+        def quantise_inc(b, q):
+            s, c = QUADRANTS[q] if q < 3 else (1, 0)
+            if ("inc_words", b) not in live:
+                live["inc_words", b] = work.tile([P, PASSES, PIXELS], U32, align_bytes=64, name="inc_words", bufs=3)
+                live["inc_scales", b] = work.tile([P, PASSES, PIXELS], U8, align_bytes=64, name="inc_scales", bufs=3)
+            cols = slice(c * HALF, (c + 1) * HALF)
             nc.vector.quantize_mx(
-                out=live["inc_words", b][:, g, :].bitcast(FP8X4),
-                scales=live["inc_scales", b][:, g, :],
-                in_=live["inc_in", b, g][:].rearrange("p w e -> p (w e)"),
+                out=live["inc_words", b][:, s, cols].bitcast(FP8X4), scales=live["inc_scales", b][:, s, cols],
+                in_=live["stage", b, q][:].rearrange("p w e -> p (w e)"),
             )
 
-        def quantise_first_pass(b, part):
+        def quantise_q0(b, part):
             quantise_inc(b, 0)
 
-        def quantise_second_pass(b, part):
+        def quantise_q1(b, part):
             quantise_inc(b, 1)
 
+        def quantise_q2(b, part):
+            quantise_inc(b, 2)
+
+        def quantise_qm(b, part):
+            quantise_inc(b, 3)
+
         def inc_times(b, g, rhs_words, rhs_scales):
-            bank = post_banks.tile([P, PACK, P], F32, tag="post")
+            bank = banks.tile([P, PACK, P], F32, tag="bank")
             for e in range(PACK):
                 cols = slice((PACK * g + e) * P, (PACK * g + e + 1) * P)
                 for s in range(PASSES):
                     nc.tensor.matmul_mx(
-                        out=bank[:, e, :],
-                        lhsT=live["inc_words", b][:, s, cols].bitcast(FP8X4),
-                        lhsT_scale=live["inc_scales", b][:, s, cols],
-                        rhs=rhs_words[:, s, :].bitcast(FP8X4),
-                        rhs_scale=rhs_scales[:, s, :],
-                        start=(s == 0),
-                        stop=(s == PASSES - 1),
+                        out=bank[:, e, :], lhsT=live["inc_words", b][:, s, cols].bitcast(FP8X4),
+                        lhsT_scale=live["inc_scales", b][:, s, cols], rhs=rhs_words[:, s, :].bitcast(FP8X4),
+                        rhs_scale=rhs_scales[:, s, :], start=(s == 0), stop=(s == PASSES - 1),
                     )
             return bank
 
@@ -239,15 +236,10 @@ def tile_hypercomputemodule_pa_t_kernel(tc, x, W_fc, b_fc, out):
         def reciprocals(b, g):
             if g == 0:
                 live["deg", b] = small.tile([P, TILES], F32, name="deg")
-            nc.vector.tensor_scalar_max(
-                out=live["deg", b][:, PACK * g : PACK * (g + 1)].unsqueeze(2),
-                in0=live["deg_ps", b, g][:, :, 0:1],
-                scalar1=1.0,
-            )
-            if g == PASSES - 1:
-                recip = small.tile([P, TILES], F32, bufs=3)
-                nc.vector.reciprocal(out=recip[:], in_=live["deg", b][:])
-                live["recip", b] = recip
+                live["recip", b] = small.tile([P, TILES], F32, name="recip")
+            cols = slice(PACK * g, PACK * (g + 1))
+            nc.vector.tensor_scalar_max(out=live["deg", b][:, cols].unsqueeze(2), in0=live["deg_ps", b, g][:, :, 0:1], scalar1=1.0)
+            nc.vector.reciprocal(out=live["recip", b][:, cols], in_=live["deg", b][:, cols])
 
         def edge_sums(b, g):
             live["edge_ps", b, g] = inc_times(b, g, live["xe_words", b], live["xe_scales", b])
@@ -272,18 +264,14 @@ def tile_hypercomputemodule_pa_t_kernel(tc, x, W_fc, b_fc, out):
             vert = work.tile([P, PACK, P], F32)
             for e in range(PACK):
                 t = PACK * g + e
-                nc.scalar.activation(
-                    out=vert[:, e, :], in_=live["vert_ps", b, g][:, e, :], func=ACT.Copy, scale=live["recip", b][:, t : t + 1]
-                )
+                nc.scalar.activation(out=vert[:, e, :], in_=live["vert_ps", b, g][:, e, :], func=ACT.Copy, scale=live["recip", b][:, t : t + 1])
             live["vert", b, g] = vert
 
         def add_x(b, g):
-            out_ps = post_banks.tile([P, PACK, P], F32, tag="post")
+            out_ps = banks.tile([P, PACK, P], F32, tag="bank")
             for e in range(PACK):
                 nc.tensor.matmul(out_ps[:, e, :], lhsT=ident_bf[:], rhs=pixel_tile(b, PACK * g + e), start=True, stop=False)
-                nc.tensor.matmul(
-                    out_ps[:, e, :], lhsT=live["vert", b, g][:, e, :], rhs=ident_f32[:], is_transpose=True, start=False, stop=True
-                )
+                nc.tensor.matmul(out_ps[:, e, :], lhsT=live["vert", b, g][:, e, :], rhs=ident_f32[:], is_transpose=True, start=False, stop=True)
             live["out_ps", b, g] = out_ps
 
         def store(b, g):
@@ -291,38 +279,41 @@ def tile_hypercomputemodule_pa_t_kernel(tc, x, W_fc, b_fc, out):
             nc.scalar.copy(out=out_sb[:], in_=live["out_ps", b, g][:].rearrange("p e w -> p (e w)"))
             nc.sync.dma_start(out=out[b].rearrange("c h w -> c (h w)")[:, g * HALF : (g + 1) * HALF], in_=out_sb[:])
 
-        def stage(i, first, parts, piece, b):
-            if first <= i < first + parts and 0 <= b < BATCH:
-                piece(b, i - first)
-
-        for b in range(-2, BATCH + 2):
-            for i in range(STEPS):
-                ahead_b, ahead_i = divmod(STEPS * b + i + AHEAD, STEPS)
-                if 0 <= ahead_b < BATCH:
-                    gram_bank(ahead_b, ahead_i)
-                if 0 <= b < BATCH:
-                    compare(b, i)
-                stage(i, 0, PACK, table_2, b)
-                stage(i, 4, PACK, table_0, b + 1)
-                stage(i, 8, PACK, table_1, b + 1)
-                stage(i, 0, 1, transpose_x, b + 2)
-                stage(i, 1, 2, square_sums, b + 2)
-                stage(i, 3, 1, h_columns, b + 2)
-                stage(i, 9, 2, spread_h, b + 2)
-                stage(i, 10, 2, copy_h, b + 2)
-                stage(i, 3, 2, project, b + 1)
-                stage(i, 4, 2, round_xe, b + 1)
-                stage(i, 6, 2, mirror, b)
-                stage(i, 7, 2, copy_mirror, b)
-                stage(i, 1, 2, vert_sums, b - 2)
-                stage(i, 2, 2, scale_vert, b - 2)
-                stage(i, 8, 2, add_x, b - 2)
-                stage(i, 9, 2, store, b - 2)
-                stage(i, 2, 2, degree_sums, b - 1)
-                stage(i, 5, 2, reciprocals, b - 1)
-                stage(i, 5, 2, edge_sums, b - 1)
-                stage(i, 8, 2, round_edge, b - 1)
-                stage(i, 10, 1, quantise_edge, b - 1)
-                stage(i, 7, 1, quantise_first_pass, b)
-                stage(i, 7, 1, quantise_xe, b + 1)
-                stage(i, 11, 1, quantise_second_pass, b)
+        PLAN = (
+            (gram_bank, tuple(range(-AHEAD, STEPS - AHEAD))),
+            (compare, tuple(range(STEPS))),
+            (reciprocals, (15, 19)),
+            (round_edge, (16, 20)),
+            (quantise_q0, (7,)),
+            (quantise_qm, (7,)),
+            (quantise_q1, (11,)),
+            (quantise_xe, (11,)),
+            (quantise_q2, (15,)),
+            (quantise_edge, (27,)),
+            (interleave_0, (4, 4, 4, 4)),
+            (interleave_1, (8, 8, 8, 8)),
+            (interleave_2, (12, 12, 12, 12)),
+            (degree_sums, (13, 17)),
+            (edge_sums, (14, 18)),
+            (mirror, (3, 4)),
+            (copy_mirror, (4, 5)),
+            (transpose_x, (-11, -10)),
+            (square_sums, (-10, -9)),
+            (spread_h, (-7, -6)),
+            (copy_h, (-6, -5)),
+            (project, (-5, -2)),
+            (round_xe, (-4, -1)),
+            (vert_sums, (32, 33)),
+            (scale_vert, (33, 34)),
+            (add_x, (35, 36)),
+            (store, (36, 37)),
+        )
+        first = min(min(p[1]) for p in PLAN)
+        last = max(max(p[1]) for p in PLAN)
+        transpose_w(0, 0)
+        for s in range(first, STEPS * (BATCH - 1) + last + 1):
+            for piece, steps in PLAN:
+                for part, start in enumerate(steps):
+                    b, rest = divmod(s - start, STEPS)
+                    if rest == 0 and 0 <= b < BATCH:
+                        piece(b, part)

@@ -24,6 +24,7 @@ QUADRANTS = ((0, 1), (0, 0), (1, 1))
 STEPS = len(QUADRANTS) * PACK
 GRAM_RING = 3
 AHEAD = GRAM_RING - 1
+SCALAR_SHARE = 128
 
 FLOPS = BATCH * (3 * 2 * PIXELS * PIXELS * P + 2 * PIXELS * P * P)
 
@@ -125,7 +126,7 @@ def tile_hypercomputemodule_pa_t_kernel(tc, x, W_fc, b_fc, out):
             live["xe_ps", b, g] = xe_ps
 
         def round_xe(b, g):
-            if g == 0:
+            if ("xe_in", b) not in live:
                 live["xe_in", b] = work.tile([P, PASSES, P, PACK], BF16, align_bytes=64, name="xe_in")
             nc.scalar.copy(out=live["xe_in", b][:, g, :, :], in_=live["xe_ps", b, g][:].rearrange("p e c -> p c e"))
 
@@ -144,6 +145,15 @@ def tile_hypercomputemodule_pa_t_kernel(tc, x, W_fc, b_fc, out):
             quantise(b, "xe")
 
         def gram_bank(b, i):
+            if b > 0 or i >= GRAM_RING:
+                fill_gram(b, i)
+
+        def first_grams(b, part):
+            if b == 0:
+                for i in range(GRAM_RING):
+                    fill_gram(b, i)
+
+        def fill_gram(b, i):
             q, e = divmod(i, PACK)
             g, c = QUADRANTS[q]
             gram = gram_banks.tile([P, HALF], F32)
@@ -176,15 +186,16 @@ def tile_hypercomputemodule_pa_t_kernel(tc, x, W_fc, b_fc, out):
                 in_=live["mirror_ps", b, pair][:].rearrange("p a e w -> p a w e"),
             )
 
-        def interleave(b, q, j):
-            if j == 0:
+        def interleave(b, q, part):
+            if ("stage", b, q) not in live:
                 live["stage", b, q] = single.tile([P, HALF, PACK], BF16, align_bytes=64, tag="stage", name="stage")
-            dst = live["stage", b, q][:, j * P : (j + 1) * P, :]
-            src = live["raw", b, q][:, :, j * P : (j + 1) * P].rearrange("p e w -> p w e")
-            if j == 0:
-                nc.scalar.copy(out=dst, in_=src)
-            else:
+            cols = slice(SCALAR_SHARE, HALF) if part == 0 else slice(0, SCALAR_SHARE)
+            dst = live["stage", b, q][:, cols, :]
+            src = live["raw", b, q][:, :, cols].rearrange("p e w -> p w e")
+            if part == 0:
                 nc.gpsimd.tensor_scalar(out=dst, in0=src, scalar1=1.0, scalar2=0.0, op0=ALU.mult, op1=ALU.add)
+            else:
+                nc.scalar.copy(out=dst, in_=src)
 
         def interleave_0(b, j):
             interleave(b, 0, j)
@@ -290,14 +301,15 @@ def tile_hypercomputemodule_pa_t_kernel(tc, x, W_fc, b_fc, out):
             (quantise_xe, (11,)),
             (quantise_q2, (15,)),
             (quantise_edge, (27,)),
-            (interleave_0, (4, 4, 4, 4)),
-            (interleave_1, (8, 8, 8, 8)),
-            (interleave_2, (12, 12, 12, 12)),
+            (interleave_0, (4, 4)),
+            (interleave_1, (8, 8)),
+            (interleave_2, (12, 12)),
             (degree_sums, (13, 17)),
             (edge_sums, (14, 18)),
             (mirror, (3, 4)),
             (copy_mirror, (4, 5)),
             (transpose_x, (-11, -10)),
+            (first_grams, (-10,)),
             (square_sums, (-10, -9)),
             (spread_h, (-7, -6)),
             (copy_h, (-6, -5)),

@@ -295,12 +295,12 @@ def tile_hypercomputemodule_pa_t_kernel(tc, x, W_fc, b_fc, out):
             (compare, tuple(range(STEPS))),
             (reciprocals, (15, 19)),
             (round_edge, (16, 20)),
-            (quantise_q0, (7,)),
             (quantise_qm, (7,)),
-            (quantise_q1, (11,)),
+            (quantise_q0, (7,)),
             (quantise_xe, (11,)),
-            (quantise_q2, (15,)),
+            (quantise_q1, (11,)),
             (quantise_edge, (27,)),
+            (quantise_q2, (15,)),
             (interleave_0, (4, 4)),
             (interleave_1, (8, 8)),
             (interleave_2, (12, 12)),

@@ -293,30 +293,30 @@ def tile_hypercomputemodule_pa_t_kernel(tc, x, W_fc, b_fc, out):
         PLAN = (
             (gram_bank, tuple(range(-AHEAD, STEPS - AHEAD))),
             (compare, tuple(range(STEPS))),
-            (reciprocals, (15, 19)),
-            (round_edge, (16, 20)),
-            (quantise_qm, (7,)),
+            (reciprocals, (16, 20)),
+            (round_edge, (16, 21)),
+            (quantise_xe, (7,)),
             (quantise_q0, (7,)),
-            (quantise_xe, (11,)),
+            (quantise_qm, (11,)),
             (quantise_q1, (11,)),
             (quantise_edge, (27,)),
             (quantise_q2, (15,)),
-            (interleave_0, (4, 4)),
-            (interleave_1, (8, 8)),
-            (interleave_2, (12, 12)),
-            (degree_sums, (13, 17)),
-            (edge_sums, (14, 18)),
-            (mirror, (3, 4)),
-            (copy_mirror, (4, 5)),
-            (transpose_x, (-11, -10)),
-            (first_grams, (-10,)),
-            (square_sums, (-10, -9)),
-            (spread_h, (-7, -6)),
-            (copy_h, (-6, -5)),
-            (project, (-5, -2)),
-            (round_xe, (-4, -1)),
-            (vert_sums, (32, 33)),
-            (scale_vert, (33, 34)),
+            (interleave_0, (4, 5)),
+            (interleave_1, (8, 9)),
+            (interleave_2, (12, 13)),
+            (degree_sums, (13, 18)),
+            (edge_sums, (14, 19)),
+            (vert_sums, (28, 29)),
+            (scale_vert, (29, 30)),
+            (mirror, (3, 8)),
+            (copy_mirror, (4, 9)),
+            (transpose_x, (-13, -12)),
+            (first_grams, (-12,)),
+            (square_sums, (-12, -11)),
+            (spread_h, (-4, -3)),
+            (copy_h, (-3, -2)),
+            (project, (-3, -2)),
+            (round_xe, (-2, -1)),
             (add_x, (35, 36)),
             (store, (36, 37)),
         )

@@ -88,7 +88,6 @@ def tile_hypercomputemodule_pa_t_kernel(tc, x, W_fc, b_fc, out):
                 live["squares", b] = work.tile([P, TILES, P], BF16, name="squares")
                 live["sq", b] = small.tile([P, TILES], F32, name="sq")
                 live["h_col", b] = small.tile([P, TILES], F32, name="h_col")
-                live["h_row", b] = work.tile([P, PIXELS], F32, name="h_row")
 
         def square_sums(b, part):
             g = 1 - part
@@ -114,6 +113,8 @@ def tile_hypercomputemodule_pa_t_kernel(tc, x, W_fc, b_fc, out):
 
         def copy_h(b, part):
             g = 1 - part
+            if ("h_row", b) not in live:
+                live["h_row", b] = work.tile([P, PIXELS], F32, name="h_row")
             nc.scalar.copy(
                 out=live["h_row", b][:, g * HALF : (g + 1) * HALF], in_=live["h_ps", b, g][:].rearrange("p e w -> p (e w)")
             )
@@ -192,7 +193,9 @@ def tile_hypercomputemodule_pa_t_kernel(tc, x, W_fc, b_fc, out):
             cols = slice(SCALAR_SHARE, HALF) if part == 0 else slice(0, SCALAR_SHARE)
             dst = live["stage", b, q][:, cols, :]
             src = live["raw", b, q][:, :, cols].rearrange("p e w -> p w e")
-            if part == 0:
+            if part == 0 and b == BATCH - 1 and q == len(QUADRANTS) - 1:
+                nc.vector.tensor_copy(out=dst, in_=src)
+            elif part == 0:
                 nc.gpsimd.tensor_scalar(out=dst, in0=src, scalar1=1.0, scalar2=0.0, op0=ALU.mult, op1=ALU.add)
             else:
                 nc.scalar.copy(out=dst, in_=src)
@@ -275,7 +278,10 @@ def tile_hypercomputemodule_pa_t_kernel(tc, x, W_fc, b_fc, out):
             vert = work.tile([P, PACK, P], F32)
             for e in range(PACK):
                 t = PACK * g + e
-                nc.scalar.activation(out=vert[:, e, :], in_=live["vert_ps", b, g][:, e, :], func=ACT.Copy, scale=live["recip", b][:, t : t + 1])
+                if b == BATCH - 1 and g == 1:
+                    nc.vector.tensor_scalar_mul(out=vert[:, e, :], in0=live["vert_ps", b, g][:, e, :], scalar1=live["recip", b][:, t : t + 1])
+                else:
+                    nc.scalar.activation(out=vert[:, e, :], in_=live["vert_ps", b, g][:, e, :], func=ACT.Copy, scale=live["recip", b][:, t : t + 1])
             live["vert", b, g] = vert
 
         def add_x(b, g):
@@ -287,38 +293,41 @@ def tile_hypercomputemodule_pa_t_kernel(tc, x, W_fc, b_fc, out):
 
         def store(b, g):
             out_sb = work.tile([P, HALF], F32)
-            nc.scalar.copy(out=out_sb[:], in_=live["out_ps", b, g][:].rearrange("p e w -> p (e w)"))
+            if b == BATCH - 1 and g == 1:
+                nc.vector.tensor_copy(out=out_sb[:], in_=live["out_ps", b, g][:].rearrange("p e w -> p (e w)"))
+            else:
+                nc.scalar.copy(out=out_sb[:], in_=live["out_ps", b, g][:].rearrange("p e w -> p (e w)"))
             nc.sync.dma_start(out=out[b].rearrange("c h w -> c (h w)")[:, g * HALF : (g + 1) * HALF], in_=out_sb[:])
 
         PLAN = (
             (gram_bank, tuple(range(-AHEAD, STEPS - AHEAD))),
             (compare, tuple(range(STEPS))),
-            (reciprocals, (16, 20)),
-            (round_edge, (16, 21)),
+            (reciprocals, (17, 20)),
+            (round_edge, (17, 21)),
+            (quantise_q2, (15,)),
             (quantise_xe, (7,)),
             (quantise_q0, (7,)),
+            (quantise_edge, (23,)),
             (quantise_qm, (11,)),
             (quantise_q1, (11,)),
-            (quantise_edge, (27,)),
-            (quantise_q2, (15,)),
             (interleave_0, (4, 5)),
             (interleave_1, (8, 9)),
             (interleave_2, (12, 13)),
-            (degree_sums, (13, 18)),
-            (edge_sums, (14, 19)),
-            (vert_sums, (28, 29)),
-            (scale_vert, (29, 30)),
-            (mirror, (3, 8)),
-            (copy_mirror, (4, 9)),
-            (transpose_x, (-13, -12)),
-            (first_grams, (-12,)),
-            (square_sums, (-12, -11)),
+            (vert_sums, (24, 25)),
+            (scale_vert, (25, 26)),
+            (degree_sums, (14, 18)),
+            (edge_sums, (15, 19)),
+            (mirror, (4, 5)),
+            (copy_mirror, (5, 6)),
+            (transpose_x, (-8, -7)),
+            (first_grams, (-7,)),
+            (square_sums, (-7, -6)),
             (spread_h, (-4, -3)),
             (copy_h, (-3, -2)),
-            (project, (-3, -2)),
-            (round_xe, (-2, -1)),
-            (add_x, (35, 36)),
-            (store, (36, 37)),
+            (add_x, (32, 33)),
+            (store, (33, 34)),
+            (project, (-2, -1)),
+            (round_xe, (-1, 0)),
         )
         first = min(min(p[1]) for p in PLAN)
         last = max(max(p[1]) for p in PLAN)

@@ -247,12 +247,15 @@ def tile_hypercomputemodule_pa_t_kernel(tc, x, W_fc, b_fc, out):
         def degree_sums(b, g):
             live["deg_ps", b, g] = inc_times(b, g, ones_words, ones_scales)
 
-        def reciprocals(b, g):
+        def clamp_degrees(b, g):
             if g == 0:
                 live["deg", b] = small.tile([P, TILES], F32, name="deg")
                 live["recip", b] = small.tile([P, TILES], F32, name="recip")
             cols = slice(PACK * g, PACK * (g + 1))
             nc.vector.tensor_scalar_max(out=live["deg", b][:, cols].unsqueeze(2), in0=live["deg_ps", b, g][:, :, 0:1], scalar1=1.0)
+
+        def reciprocals(b, g):
+            cols = slice(PACK * g, PACK * (g + 1))
             nc.vector.reciprocal(out=live["recip", b][:, cols], in_=live["deg", b][:, cols])
 
         def edge_sums(b, g):
@@ -302,8 +305,9 @@ def tile_hypercomputemodule_pa_t_kernel(tc, x, W_fc, b_fc, out):
         PLAN = (
             (gram_bank, tuple(range(-AHEAD, STEPS - AHEAD))),
             (compare, tuple(range(STEPS))),
-            (reciprocals, (17, 20)),
-            (round_edge, (17, 21)),
+            (clamp_degrees, (16, 20)),
+            (reciprocals, (17, 21)),
+            (round_edge, (18, 22)),
             (quantise_q2, (15,)),
             (quantise_xe, (7,)),
             (quantise_q0, (7,)),

@@ -42,7 +42,8 @@ def tile_hypercomputemodule_pa_t_kernel(tc, x, W_fc, b_fc, out):
 
         x_sb = consts.tile([P, BATCH, PIXELS], BF16)
         for b in range(BATCH):
-            nc.sync.dma_start(out=x_sb[:, b, :], in_=x[b].rearrange("c h w -> c (h w)"))
+            for g in (1, 0):
+                nc.sync.dma_start(out=x_sb[:, b, g * HALF : (g + 1) * HALF], in_=x[b].rearrange("c h w -> c (h w)")[:, g * HALF : (g + 1) * HALF])
         w_sb = consts.tile([P, P], BF16)
         nc.scalar.dma_start(out=w_sb[:], in_=W_fc)
         bias_rows = consts.tile([P, P], BF16)
@@ -290,8 +291,11 @@ def tile_hypercomputemodule_pa_t_kernel(tc, x, W_fc, b_fc, out):
         def add_x(b, g):
             out_ps = banks.tile([P, PACK, P], F32, tag="bank")
             for e in range(PACK):
-                nc.tensor.matmul(out_ps[:, e, :], lhsT=ident_bf[:], rhs=pixel_tile(b, PACK * g + e), start=True, stop=False)
-                nc.tensor.matmul(out_ps[:, e, :], lhsT=live["vert", b, g][:, e, :], rhs=ident_f32[:], is_transpose=True, start=False, stop=True)
+                for turn in range(2):
+                    if turn == e % 2:
+                        nc.tensor.matmul(out_ps[:, e, :], lhsT=live["vert", b, g][:, e, :], rhs=ident_f32[:], is_transpose=True, start=(turn == 0), stop=(turn == 1))
+                    else:
+                        nc.tensor.matmul(out_ps[:, e, :], lhsT=ident_bf[:], rhs=pixel_tile(b, PACK * g + e), start=(turn == 0), stop=(turn == 1))
             live["out_ps", b, g] = out_ps
 
         def store(b, g):

from contextlib import ExitStack

import concourse.mybir as mybir
from concourse.masks import make_identity

F32 = mybir.dt.float32
BF16 = mybir.dt.bfloat16
U32 = mybir.dt.uint32
U8 = mybir.dt.uint8
FP8X4 = mybir.dt.float8_e4m3fn_x4
ALU = mybir.AluOpType
ACT = mybir.ActivationFunctionType

P = 128
BATCH = 8
PIXELS = 1024
TILES = PIXELS // P
PACK = 4
PASSES = TILES // PACK
HALF = PACK * P
THRESHOLD = 16.0
RUN = 4
QUADRANTS = ((0, 1), (0, 0), (1, 1))
STEPS = len(QUADRANTS) * PACK
GRAM_RING = 3
AHEAD = GRAM_RING - 1
SCALAR_SHARE = 128

FLOPS = BATCH * (3 * 2 * PIXELS * PIXELS * P + 2 * PIXELS * P * P)


def tile_hypercomputemodule_pa_t_kernel(tc, x, W_fc, b_fc, out):
    nc = tc.nc
    with ExitStack() as ctx:
        consts = ctx.enter_context(tc.tile_pool(name="consts", bufs=1))
        small = ctx.enter_context(tc.tile_pool(name="small", bufs=3))
        work = ctx.enter_context(tc.tile_pool(name="work", bufs=2))
        single = ctx.enter_context(tc.tile_pool(name="single", bufs=1))
        gram_banks = ctx.enter_context(tc.psum_pool(name="gram_banks", bufs=GRAM_RING))
        banks = ctx.enter_context(tc.psum_pool(name="banks", bufs=8 - GRAM_RING))
        ctx.enter_context(tc.manual_schedule())

        x_sb = consts.tile([P, BATCH, PIXELS], BF16)
        for b in range(BATCH):
            for g in (1, 0):
                nc.sync.dma_start(out=x_sb[:, b, g * HALF : (g + 1) * HALF], in_=x[b].rearrange("c h w -> c (h w)")[:, g * HALF : (g + 1) * HALF])
        w_sb = consts.tile([P, P], BF16)
        nc.scalar.dma_start(out=w_sb[:], in_=W_fc)
        bias_rows = consts.tile([P, P], BF16)
        nc.vector.memset(bias_rows[:], 0.0)
        nc.scalar.dma_start(out=bias_rows[0:1, :], in_=b_fc.rearrange("(o c) -> o c", o=1))
        ones_bf = consts.tile([P, P], BF16)
        nc.vector.memset(ones_bf[:], 1.0)
        warm = consts.tile([P, 1], F32)
        nc.scalar.activation(out=warm[:], in_=ones_bf[:, 0:1], func=ACT.Square)
        ident_bf = consts.tile([P, P], BF16)
        make_identity(nc, ident_bf[:])
        ident_f32 = consts.tile([P, P], F32)
        make_identity(nc, ident_f32[:])

        ones_in = consts.tile([P, PASSES * P * PACK], BF16, align_bytes=64)
        nc.vector.memset(ones_in[:], 1.0)
        ones_words = consts.tile([P, PASSES, P], U32, align_bytes=64)
        ones_scales = consts.tile([P, PASSES, P], U8, align_bytes=64)
        nc.vector.quantize_mx(
            out=ones_words[:].rearrange("p g c -> p (g c)").bitcast(FP8X4),
            scales=ones_scales[:].rearrange("p g c -> p (g c)"),
            in_=ones_in[:],
        )
        w_t = consts.tile([P, P], BF16)

        live = {}

        def pixel_tile(b, t):
            return x_sb[:, b, t * P : (t + 1) * P]

        def transpose_w(b, part):
            w_ps = banks.tile([P, P], BF16, tag="bank")
            nc.tensor.transpose(w_ps[:], w_sb[:], ident_bf[:])
            nc.vector.tensor_copy(out=w_t[:], in_=w_ps[:])

        def transpose_x(b, part):
            g = 1 - part
            xf_ps = banks.tile([P, PACK, P], BF16, tag="bank")
            for e in range(PACK):
                nc.tensor.transpose(xf_ps[:, e, :], pixel_tile(b, PACK * g + e), ident_bf[:])
            live["xf_ps", b, g] = xf_ps
            if part == 0:
                live["squares", b] = work.tile([P, TILES, P], BF16, name="squares")
                live["sq", b] = small.tile([P, TILES], F32, name="sq")
                live["h_col", b] = small.tile([P, TILES], F32, name="h_col")

        def square_sums(b, part):
            g = 1 - part
            for e in range(PACK):
                t = PACK * g + e
                nc.scalar.activation(
                    out=live["squares", b][:, t, :], in_=live["xf_ps", b, g][:, e, :], func=ACT.Square,
                    accum_out=live["sq", b][:, t : t + 1],
                )
            cols = slice(PACK * g, PACK * (g + 1))
            nc.scalar.activation(
                out=live["h_col", b][:, cols], in_=live["sq", b][:, cols], func=ACT.Copy, scale=0.5,
                bias=-THRESHOLD * THRESHOLD / 4.0,
            )

        def spread_h(b, part):
            g = 1 - part
            h_ps = banks.tile([P, PACK, P], F32, tag="bank")
            for e in range(PACK):
                t = PACK * g + e
                nc.tensor.transpose(h_ps[:, e, :], live["h_col", b][:, t : t + 1].to_broadcast([P, P]), ident_f32[:])
            live["h_ps", b, g] = h_ps

        def copy_h(b, part):
            g = 1 - part
            if ("h_row", b) not in live:
                live["h_row", b] = work.tile([P, PIXELS], F32, name="h_row")
            nc.scalar.copy(
                out=live["h_row", b][:, g * HALF : (g + 1) * HALF], in_=live["h_ps", b, g][:].rearrange("p e w -> p (e w)")
            )

        def project(b, g):
            xe_ps = banks.tile([P, PACK, P], F32, tag="bank")
            for e in range(PACK):
                nc.tensor.matmul(xe_ps[:, e, :], lhsT=ones_bf[:], rhs=bias_rows[:], start=True, stop=False)
                nc.tensor.matmul(xe_ps[:, e, :], lhsT=pixel_tile(b, PACK * g + e), rhs=w_t[:], start=False, stop=True)
            live["xe_ps", b, g] = xe_ps

        def round_xe(b, g):
            if ("xe_in", b) not in live:
                live["xe_in", b] = work.tile([P, PASSES, P, PACK], BF16, align_bytes=64, name="xe_in")
            nc.scalar.copy(out=live["xe_in", b][:, g, :, :], in_=live["xe_ps", b, g][:].rearrange("p e c -> p c e"))

        def quantise(b, name):
            words = work.tile([P, PASSES, P], U32, align_bytes=64, name=name + "_words", bufs=3)
            scales = work.tile([P, PASSES, P], U8, align_bytes=64, name=name + "_scales", bufs=3)
            nc.vector.quantize_mx(
                out=words[:].rearrange("p g c -> p (g c)").bitcast(FP8X4),
                scales=scales[:].rearrange("p g c -> p (g c)"),
                in_=live[name + "_in", b][:].rearrange("p g c e -> p (g c e)"),
            )
            live[name + "_words", b] = words
            live[name + "_scales", b] = scales

        def quantise_xe(b, part):
            quantise(b, "xe")

        def gram_bank(b, i):
            if b > 0 or i >= GRAM_RING:
                fill_gram(b, i)

        def first_grams(b, part):
            if b == 0:
                for i in range(GRAM_RING):
                    fill_gram(b, i)

        def fill_gram(b, i):
            q, e = divmod(i, PACK)
            g, c = QUADRANTS[q]
            gram = gram_banks.tile([P, HALF], F32)
            nc.tensor.matmul(gram[:], lhsT=pixel_tile(b, PACK * g + e), rhs=x_sb[:, b, c * HALF : (c + 1) * HALF], start=True, stop=True)
            live["gram", b, i] = gram

        def compare(b, i):
            q, e = divmod(i, PACK)
            g, c = QUADRANTS[q]
            if e == 0:
                live["raw", b, q] = single.tile([P, PACK, HALF], BF16, tag="raw%d" % q, name="raw")
            t = PACK * g + e
            nc.vector.scalar_tensor_tensor(
                out=live["raw", b, q][:, e, :], in0=live["gram", b, i][:], scalar=live["h_col", b][:, t : t + 1],
                in1=live["h_row", b][:, c * HALF : (c + 1) * HALF], op0=ALU.subtract, op1=ALU.is_gt,
            )

        def mirror(b, pair):
            mirror_ps = banks.tile([P, 2, PACK, P], BF16, tag="bank")
            for a in range(2):
                for e in range(PACK):
                    nc.tensor.transpose(mirror_ps[:, a, e, :], live["raw", b, 0][:, 2 * pair + a, e * P : (e + 1) * P], ident_bf[:])
            live["mirror_ps", b, pair] = mirror_ps

        def copy_mirror(b, pair):
            if pair == 0:
                live["stage", b, 3] = single.tile([P, HALF, PACK], BF16, align_bytes=64, tag="stage_m", name="stage_m")
            nc.scalar.copy(
                out=live["stage", b, 3][:, 2 * pair * P : 2 * (pair + 1) * P, :].rearrange("p (a w) e -> p a w e", a=2),
                in_=live["mirror_ps", b, pair][:].rearrange("p a e w -> p a w e"),
            )

        def interleave(b, q, part):
            if ("stage", b, q) not in live:
                live["stage", b, q] = single.tile([P, HALF, PACK], BF16, align_bytes=64, tag="stage", name="stage")
            cols = slice(SCALAR_SHARE, HALF) if part == 0 else slice(0, SCALAR_SHARE)
            dst = live["stage", b, q][:, cols, :]
            src = live["raw", b, q][:, :, cols].rearrange("p e w -> p w e")
            if part == 0 and b == BATCH - 1 and q == len(QUADRANTS) - 1:
                nc.vector.tensor_copy(out=dst, in_=src)
            elif part == 0:
                nc.gpsimd.tensor_scalar(out=dst, in0=src, scalar1=1.0, scalar2=0.0, op0=ALU.mult, op1=ALU.add)
            else:
                nc.scalar.copy(out=dst, in_=src)

        def interleave_0(b, j):
            interleave(b, 0, j)

        def interleave_1(b, j):
            interleave(b, 1, j)

        def interleave_2(b, j):
            interleave(b, 2, j)

        def quantise_inc(b, q):
            s, c = QUADRANTS[q] if q < 3 else (1, 0)
            if ("inc_words", b) not in live:
                live["inc_words", b] = work.tile([P, PASSES, PIXELS], U32, align_bytes=64, name="inc_words", bufs=3)
                live["inc_scales", b] = work.tile([P, PASSES, PIXELS], U8, align_bytes=64, name="inc_scales", bufs=3)
            cols = slice(c * HALF, (c + 1) * HALF)
            nc.vector.quantize_mx(
                out=live["inc_words", b][:, s, cols].bitcast(FP8X4), scales=live["inc_scales", b][:, s, cols],
                in_=live["stage", b, q][:].rearrange("p w e -> p (w e)"),
            )

        def quantise_q0(b, part):
            quantise_inc(b, 0)

        def quantise_q1(b, part):
            quantise_inc(b, 1)

        def quantise_q2(b, part):
            quantise_inc(b, 2)

        def quantise_qm(b, part):
            quantise_inc(b, 3)

        def inc_times(b, g, rhs_words, rhs_scales):
            bank = banks.tile([P, PACK, P], F32, tag="bank")
            for e in range(PACK):
                cols = slice((PACK * g + e) * P, (PACK * g + e + 1) * P)
                for s in range(PASSES):
                    nc.tensor.matmul_mx(
                        out=bank[:, e, :], lhsT=live["inc_words", b][:, s, cols].bitcast(FP8X4),
                        lhsT_scale=live["inc_scales", b][:, s, cols], rhs=rhs_words[:, s, :].bitcast(FP8X4),
                        rhs_scale=rhs_scales[:, s, :], start=(s == 0), stop=(s == PASSES - 1),
                    )
            return bank

        def degree_sums(b, g):
            live["deg_ps", b, g] = inc_times(b, g, ones_words, ones_scales)

        def clamp_degrees(b, g):
            if g == 0:
                live["deg", b] = small.tile([P, TILES], F32, name="deg")
                live["recip", b] = small.tile([P, TILES], F32, name="recip")
            cols = slice(PACK * g, PACK * (g + 1))
            nc.vector.tensor_scalar_max(out=live["deg", b][:, cols].unsqueeze(2), in0=live["deg_ps", b, g][:, :, 0:1], scalar1=1.0)

        def reciprocals(b, g):
            cols = slice(PACK * g, PACK * (g + 1))
            nc.vector.reciprocal(out=live["recip", b][:, cols], in_=live["deg", b][:, cols])

        def edge_sums(b, g):
            live["edge_ps", b, g] = inc_times(b, g, live["xe_words", b], live["xe_scales", b])

        def round_edge(b, g):
            if g == 0:
                live["edge_in", b] = work.tile([P, PASSES, P, PACK], BF16, align_bytes=64, name="edge_in")
            nc.vector.tensor_tensor(
                out=live["edge_in", b][:, g, :, :].rearrange("p (r i) e -> p r e i", i=RUN),
                in0=live["edge_ps", b, g][:].rearrange("p e (r i) -> p r e i", i=RUN),
                in1=live["recip", b][:, PACK * g : PACK * (g + 1)].unsqueeze(1).unsqueeze(3).to_broadcast([P, P // RUN, PACK, RUN]),
                op=ALU.mult,
            )

        def quantise_edge(b, part):
            quantise(b, "edge")

        def vert_sums(b, g):
            live["vert_ps", b, g] = inc_times(b, g, live["edge_words", b], live["edge_scales", b])

        def scale_vert(b, g):
            vert = work.tile([P, PACK, P], F32)
            for e in range(PACK):
                t = PACK * g + e
                if b == BATCH - 1 and g == 1:
                    nc.vector.tensor_scalar_mul(out=vert[:, e, :], in0=live["vert_ps", b, g][:, e, :], scalar1=live["recip", b][:, t : t + 1])
                else:
                    nc.scalar.activation(out=vert[:, e, :], in_=live["vert_ps", b, g][:, e, :], func=ACT.Copy, scale=live["recip", b][:, t : t + 1])
            live["vert", b, g] = vert

        def add_x(b, g):
            out_ps = banks.tile([P, PACK, P], F32, tag="bank")
            for e in range(PACK):
                for turn in range(2):
                    if turn == e % 2:
                        nc.tensor.matmul(out_ps[:, e, :], lhsT=live["vert", b, g][:, e, :], rhs=ident_f32[:], is_transpose=True, start=(turn == 0), stop=(turn == 1))
                    else:
                        nc.tensor.matmul(out_ps[:, e, :], lhsT=ident_bf[:], rhs=pixel_tile(b, PACK * g + e), start=(turn == 0), stop=(turn == 1))
            live["out_ps", b, g] = out_ps

        def store(b, g):
            out_sb = work.tile([P, HALF], F32)
            if b == BATCH - 1 and g == 1:
                nc.vector.tensor_copy(out=out_sb[:], in_=live["out_ps", b, g][:].rearrange("p e w -> p (e w)"))
            else:
                nc.scalar.copy(out=out_sb[:], in_=live["out_ps", b, g][:].rearrange("p e w -> p (e w)"))
            nc.sync.dma_start(out=out[b].rearrange("c h w -> c (h w)")[:, g * HALF : (g + 1) * HALF], in_=out_sb[:])

        PLAN = (
            (gram_bank, tuple(range(-AHEAD, STEPS - AHEAD))),
            (compare, tuple(range(STEPS))),
            (clamp_degrees, (16, 20)),
            (reciprocals, (17, 21)),
            (round_edge, (18, 22)),
            (quantise_q2, (15,)),
            (quantise_xe, (7,)),
            (quantise_q0, (7,)),
            (quantise_edge, (23,)),
            (quantise_qm, (11,)),
            (quantise_q1, (11,)),
            (interleave_0, (4, 5)),
            (interleave_1, (8, 9)),
            (interleave_2, (12, 13)),
            (vert_sums, (24, 25)),
            (scale_vert, (25, 26)),
            (degree_sums, (14, 18)),
            (edge_sums, (15, 19)),
            (mirror, (4, 5)),
            (copy_mirror, (5, 6)),
            (transpose_x, (-8, -7)),
            (first_grams, (-7,)),
            (square_sums, (-7, -6)),
            (spread_h, (-4, -3)),
            (copy_h, (-3, -2)),
            (add_x, (32, 33)),
            (store, (33, 34)),
            (project, (-2, -1)),
            (round_xe, (-1, 0)),
        )
        first = min(min(p[1]) for p in PLAN)
        last = max(max(p[1]) for p in PLAN)
        transpose_w(0, 0)
        for s in range(first, STEPS * (BATCH - 1) + last + 1):
            for piece, steps in PLAN:
                for part, start in enumerate(steps):
                    b, rest = divmod(s - start, STEPS)
                    if rest == 0 and 0 <= b < BATCH:
                        piece(b, part)
